import numpy as np
import ml_dtypes


def mxq(x, axis, fmt="e4m3"):
    dtype, down = {"e4m3": (ml_dtypes.float8_e4m3fn, 7), "e5m2": (ml_dtypes.float8_e5m2, 14)}[fmt]
    v = np.moveaxis(np.asarray(x, np.float32).astype(ml_dtypes.bfloat16).astype(np.float64), axis, -1)
    blocks = v.reshape(v.shape[:-1] + (-1, 32))
    amax = np.abs(blocks).max(-1, keepdims=True)
    byte = np.maximum(np.where(amax > 0, np.frexp(amax)[1] - 1 + 127, 0) - down, 1)
    scale = np.exp2(byte - 127.0)
    codes = (blocks / scale).astype(np.float32).astype(dtype).astype(np.float64)
    return np.moveaxis((codes * scale).reshape(v.shape), -1, axis)


WIDE = False


def mx_kscale(k):
    if not WIDE:
        return np.ones(k)
    levels = np.array([10, -10, 5, -5, 0])
    a = np.random.permutation(np.resize(levels, k // 512 * 4)).reshape(k // 512, 4)
    idx = np.arange(k)
    return np.exp2(a[idx // 512, idx % 128 // 32])


BF16 = ml_dtypes.bfloat16


def bf(x):
    return np.asarray(x, np.float32).astype(BF16)


def f64(x):
    return np.asarray(x).astype(np.float64)


B, T, C, CO, HS, DW, DA, DV, DG = 8, 1024, 1024, 256, 64, 128, 128, 128, 256


def sigmoid(u):
    return 1.0 / (1.0 + np.exp(-u))


def setup_inputs():
    n = np.random.standard_normal
    s = mx_kscale(C)
    return {
        "x": bf(n((B, T, C)) * s),
        "x_v": bf(n((1, 1, C)) * 0.3),
        "W_v": bf(n((CO, C)) / np.sqrt(C) / s),
        "v_hid": bf(n((B, T, DV))),
        "v2": bf(n((DV, CO)) / np.sqrt(DV)),
        "v0": bf(0.73 + n((1, 1, CO)) * 0.2),
        "v_first": bf(n((B, T, CO))),
    }


def reference(x, x_v, W_v, v_hid, v2, v0, v_first):
    x = f64(x)
    prev = np.concatenate([np.zeros_like(x[:, :1]), x[:, :-1]], axis=1)
    xv = x + (prev - x) * f64(x_v)
    v = mxq(xv, 2, "e4m3") @ mxq(f64(W_v), 1, "e4m3").T
    mix = sigmoid(f64(v0) + f64(v_hid) @ f64(v2))
    return v + (f64(v_first) - v) * mix

@@ -1,0 +1,303 @@
+from contextlib import ExitStack
+
+import concourse.mybir as mybir
+from concourse.masks import make_identity
+
+FP8X4 = mybir.dt.float8_e4m3fn_x4
+BF16 = mybir.dt.bfloat16
+F32 = mybir.dt.float32
+U32 = mybir.dt.uint32
+U8 = mybir.dt.uint8
+ALU = mybir.AluOpType
+ACT = mybir.ActivationFunctionType
+
+P = 128
+B, T, C, CO, DV = 8, 1024, 1024, 256, 128
+FLOPS = 2 * B * T * C * CO + 2 * B * T * DV * CO
+
+N_STEPS = 4 * B
+L_ORDER = (3, 0, 1, 2)
+NG = 128
+X_AHEAD = 5
+
+
+def planes():
+    return [(g, u, e) for g in range(2) for u in range(2) for e in range(2)]
+
+
+def tile_full_tmix_params_pb_t_kernel(tc, x, x_v, W_v, v_hid, v2, v0, v_first, out):
+    nc = tc.nc
+    with ExitStack() as ctx:
+        const = ctx.enter_context(tc.tile_pool(name="const", bufs=1))
+        xin = ctx.enter_context(tc.tile_pool(name="xin", bufs=X_AHEAD + 1))
+        seqp = ctx.enter_context(tc.tile_pool(name="seqp", bufs=3))
+        work = ctx.enter_context(tc.tile_pool(name="work", bufs=3))
+        ep = ctx.enter_context(tc.tile_pool(name="ep", bufs=3))
+        psum = ctx.enter_context(tc.psum_pool(name="psum", bufs=1))
+
+        def l_key(k):
+            return (k // 4, L_ORDER[k % 4])
+
+        x_tiles = {}
+
+        def load_x(k):
+            b, s = l_key(k)
+            x_sb = xin.tile([P, 2, C], BF16, name="x_sb")
+            src = x[b].rearrange("(p i s) c -> p i s c", i=2, s=4)
+            nc.sync.dma_start(out=x_sb[:], in_=src[:, :, s, :])
+            x_tiles[k] = x_sb
+
+        seq_tiles = {}
+
+        def load_seq(b):
+            vh = seqp.tile([P, 8, DV], BF16, name="vh")
+            nc.sync.dma_start(out=vh[:], in_=v_hid[b].rearrange("(p j) d -> p j d", j=8))
+            vf = seqp.tile([P, 8, CO], BF16, name="vf")
+            nc.sync.dma_start(out=vf[:], in_=v_first[b].rearrange("(p j) c -> p j c", j=8))
+            seq_tiles[b] = (vh, vf)
+
+        xv_rows = const.tile([P, P], F32, name="xv_rows")
+        nc.vector.memset(xv_rows[:], 0.0)
+        nc.sync.dma_start(
+            out=xv_rows[:].bitcast(BF16)[0:4, :],
+            in_=x_v.rearrange("a b (r c) -> (a b r) c", r=4),
+        )
+        load_x(0)
+        load_x(1)
+        w_sb = const.tile([P, 2, C], BF16, name="w_sb")
+        nc.sync.dma_start(out=w_sb[:], in_=W_v.rearrange("(h p) c -> p h c", p=P))
+        v0_row = const.tile([P, CO], BF16, name="v0_row")
+        nc.vector.memset(v0_row[:], 0.0)
+        nc.sync.dma_start(out=v0_row[0:1, :], in_=v0.rearrange("a b c -> (a b) c"))
+        v2_sb = const.tile([P, CO], BF16, name="v2_sb")
+        nc.sync.dma_start(out=v2_sb[:], in_=v2)
+        load_seq(0)
+        for k in range(2, X_AHEAD):
+            load_x(k)
+
+        ident_f = const.tile([P, P], F32, name="ident_f")
+        make_identity(nc, ident_f[:])
+        ident_b = const.tile([P, P], BF16, name="ident_b")
+        make_identity(nc, ident_b[:])
+        ones = const.tile([P, P], BF16, name="ones")
+        nc.vector.memset(ones[:], 1.0)
+
+        xv_ps = psum.tile([P, 2, 2, P], F32, tag="xt", bufs=4, name="xv_ps")
+        nc.tensor.transpose(xv_ps[:, 0, 0, :], xv_rows[:], ident_f[:])
+        m = const.tile([P, 8], F32, name="m")
+        nc.vector.tensor_copy(out=m[:], in_=xv_ps[:, 0, 0, 0:4].bitcast(BF16))
+        om = const.tile([P, 8], F32, name="om")
+        nc.vector.tensor_scalar(
+            out=om[:], in0=m[:], scalar1=-1.0, scalar2=1.0, op0=ALU.mult, op1=ALU.add
+        )
+
+        def prepare_w():
+            w_words = w_sb[:].bitcast(F32)
+            w_grp = const.tile([P, 2, CO, 4], BF16, name="w_grp", align_bytes=64)
+            w_grp_words = w_grp[:].bitcast(F32)
+            for g in range(2):
+                w_ps = psum.tile([P, 2, 2, P], F32, tag="xt", bufs=4, name="w_ps")
+                for u in range(2):
+                    for h in range(2):
+                        c0 = (2 * g + u) * P
+                        nc.tensor.transpose(w_ps[:, u, h, :], w_words[:, h, c0 : c0 + P], ident_f[:])
+                nc.vector.tensor_copy(
+                    out=w_grp_words[:, g, :, :], in_=w_ps[:].rearrange("p u h r -> p (h r) u")
+                )
+            w_codes = const.tile([P, 2 * CO], U32, name="w_codes", align_bytes=64)
+            w_scales = const.tile([P, 2 * CO], U8, name="w_scales", align_bytes=64)
+            nc.vector.quantize_mx(
+                out=w_codes[:].bitcast(FP8X4),
+                scales=w_scales[:],
+                in_=w_grp[:].rearrange("p g c t -> p (g c t)"),
+            )
+            return w_codes, w_scales
+
+        def prepare_bias():
+            b_ps = psum.tile([P, 2, CO], F32, tag="g", bufs=1, name="b_ps")
+            nc.tensor.matmul(out=b_ps[:, 0, :], lhsT=ones[:], rhs=v0_row[:], start=True, stop=True)
+            v0_b = const.tile([P, CO], F32, name="v0_b")
+            nc.vector.tensor_copy(out=v0_b[:], in_=b_ps[:, 0, :])
+            return v0_b
+
+        vht_tiles = {}
+
+        def prepare_vht(b):
+            vh = seq_tiles[b][0]
+            vh_ps = psum.tile([P, 8, P], BF16, tag="st", bufs=1, name="vh_ps")
+            for j in range(8):
+                nc.tensor.transpose(vh_ps[:, j, :], vh[:, j, :], ident_b[:])
+            vht = seqp.tile([P, 8, P], BF16, name="vht")
+            nc.scalar.copy(out=vht[:], in_=vh_ps[:])
+            vht_tiles[b] = vht
+
+        banks = {}
+        a_tiles = {}
+
+        def stage_l(k):
+            key = l_key(k)
+            xw = x_tiles[k][:].bitcast(F32)
+            if key[1] == 3:
+                a = work.tile([P, 8, 2, P], F32, tag="a3", bufs=2, name="a3")
+            else:
+                a = work.tile([P, 8, 2, P], F32, tag="a", bufs=3, name="a")
+            views = []
+            for g in range(2):
+                bk = psum.tile([P, 2, 2, P], F32, tag="xt", bufs=4, name="xt_ps")
+                for u in range(2):
+                    for i in range(2):
+                        c0 = (2 * g + u) * P
+                        nc.tensor.transpose(bk[:, u, i, :], xw[:, i, c0 : c0 + P], ident_f[:])
+                bv = bk[:].bitcast(BF16).rearrange("p u i (r e) -> p u i r e", e=2)
+                for u in range(2):
+                    for e in range(2):
+                        pl = 4 * g + 2 * u + e
+                        nc.scalar.activation(
+                            out=a[:, pl, :, :],
+                            in_=bv[:, u, :, :, e],
+                            func=ACT.Copy,
+                            scale=om[:, pl : pl + 1],
+                        )
+                views.append(bv)
+            banks[key] = views
+            a_tiles[key] = a
+
+        xvp_tiles = {}
+
+        def stage_mix(n):
+            b, s = n // 4, n % 4
+            prev = banks[(b, (s + 3) % 4)]
+            a = a_tiles[(b, s)]
+            xvp = work.tile([P, 8, 2, P], BF16, name="xvp")
+            for g, u, e in planes():
+                pl = 4 * g + 2 * u + e
+                sc = m[:, pl : pl + 1]
+                if s > 0:
+                    nc.vector.scalar_tensor_tensor(
+                        out=xvp[:, pl, :, :], in0=prev[g][:, u, :, :, e], scalar=sc,
+                        in1=a[:, pl, :, :], op0=ALU.mult, op1=ALU.add,
+                    )
+                else:
+                    nc.vector.scalar_tensor_tensor(
+                        out=xvp[:, pl, 0, 1:P], in0=prev[g][:, u, 1, 0 : P - 1, e], scalar=sc,
+                        in1=a[:, pl, 0, 1:P], op0=ALU.mult, op1=ALU.add,
+                    )
+                    nc.vector.scalar_tensor_tensor(
+                        out=xvp[:, pl, 1, :], in0=prev[g][:, u, 0, :, e], scalar=sc,
+                        in1=a[:, pl, 1, :], op0=ALU.mult, op1=ALU.add,
+                    )
+            if s == 0:
+                nc.vector.tensor_copy(out=xvp[:, :, 0, 0:1], in_=a[:, :, 0, 0:1])
+            xvp_tiles[n] = xvp
+
+        grp_tiles = {}
+
+        def stage_regroup(n):
+            xvp = xvp_tiles[n]
+            grp = work.tile([P, 2, 2 * P, 4], BF16, name="grp", align_bytes=64)
+            src = xvp[:].rearrange("p (g t) i r -> p g (i r) t", g=2)
+            nc.gpsimd.tensor_scalar(
+                out=grp[:, 0, :, :], in0=src[:, 0, :, :], scalar1=1.0, scalar2=0.0,
+                op0=ALU.mult, op1=ALU.add,
+            )
+            nc.gpsimd.tensor_scalar(
+                out=grp[:, 1, 0:NG, :], in0=src[:, 1, 0:NG, :], scalar1=1.0, scalar2=0.0,
+                op0=ALU.mult, op1=ALU.add,
+            )
+            nc.scalar.copy(out=grp[:, 1, NG:, :], in_=src[:, 1, NG:, :])
+            grp_tiles[n] = grp
+
+        g_tiles = {}
+
+        def stage_gate(n):
+            b, s = n // 4, n % 4
+            vht = vht_tiles[b]
+            g_ps = psum.tile([P, 2, CO], F32, tag="g", bufs=1, name="g_ps")
+            on_pe = n % 2 == 0
+            for i in range(2):
+                if on_pe:
+                    nc.tensor.matmul(out=g_ps[:, i, :], lhsT=ones[:], rhs=v0_row[:], start=True, stop=False)
+                nc.tensor.matmul(
+                    out=g_ps[:, i, :], lhsT=vht[:, 4 * i + s, :], rhs=v2_sb[:],
+                    start=not on_pe, stop=True,
+                )
+            g_tiles[n] = g_ps
+
+        mix_tiles = {}
+
+        def stage_sigmoid(n):
+            g_ps = g_tiles[n]
+            mix = ep.tile([P, 2, CO], F32, name="mix")
+            if n % 2 == 0:
+                nc.scalar.activation(out=mix[:], in_=g_ps[:], func=ACT.Sigmoid)
+            else:
+                u_sb = ep.tile([P, 2, CO], F32, name="u_sb")
+                nc.vector.tensor_tensor(
+                    out=u_sb[:], in0=g_ps[:], in1=v0_b[:].unsqueeze(1).to_broadcast([P, 2, CO]),
+                    op=ALU.add,
+                )
+                nc.scalar.activation(out=mix[:], in_=u_sb[:], func=ACT.Sigmoid)
+            mix_tiles[n] = mix
+
+        v_tiles = {}
+
+        def stage_mx(n):
+            grp = grp_tiles[n]
+            xc = work.tile([P, 4 * P], U32, name="xc", align_bytes=64)
+            xs = work.tile([P, 4 * P], U8, name="xs", align_bytes=64)
+            nc.vector.quantize_mx(
+                out=xc[:].bitcast(FP8X4), scales=xs[:], in_=grp[:].rearrange("p g n t -> p (g n t)")
+            )
+            v_ps = psum.tile([P, 2, CO], F32, tag="v", bufs=2, name="v_ps")
+            for i in range(2):
+                for g in range(2):
+                    c0 = g * 2 * P + i * P
+                    nc.tensor.matmul_mx(
+                        out=v_ps[:, i, :],
+                        lhsT=xc[:, c0 : c0 + P].bitcast(FP8X4),
+                        lhsT_scale=xs[:, c0 : c0 + P],
+                        rhs=w_codes[:, g * CO : (g + 1) * CO].bitcast(FP8X4),
+                        rhs_scale=w_scales[:, g * CO : (g + 1) * CO],
+                        start=(g == 0),
+                        stop=(g == 1),
+                    )
+            v_tiles[n] = v_ps
+
+        def stage_blend(n):
+            b, s = n // 4, n % 4
+            v_ps = v_tiles[n]
+            mix = mix_tiles[n]
+            vf = seq_tiles[b][1][:].rearrange("p (i s) c -> p i s c", s=4)[:, :, s, :]
+            e_sb = ep.tile([P, 2, CO], F32, name="e_sb")
+            nc.vector.tensor_tensor(out=e_sb[:], in0=vf, in1=v_ps[:], op=ALU.subtract)
+            f_sb = ep.tile([P, 2, CO], F32, name="f_sb")
+            nc.gpsimd.tensor_tensor(out=f_sb[:], in0=e_sb[:], in1=mix[:], op=ALU.mult)
+            o_sb = ep.tile([P, 2, CO], F32, name="o_sb")
+            nc.vector.tensor_tensor(out=o_sb[:], in0=f_sb[:], in1=v_ps[:], op=ALU.add)
+            dst = out[b].rearrange("(p i s) c -> p i s c", i=2, s=4)
+            nc.sync.dma_start(out=dst[:, :, s, :], in_=o_sb[:])
+
+        stage_l(0)
+        w_codes, w_scales = prepare_w()
+        v0_b = prepare_bias()
+        prepare_vht(0)
+        for n in range(N_STEPS + 2):
+            if n + X_AHEAD < N_STEPS:
+                load_x(n + X_AHEAD)
+            if n % 4 == 0 and n // 4 + 1 < B:
+                load_seq(n // 4 + 1)
+            if n + 1 < N_STEPS:
+                stage_l(n + 1)
+            if n < N_STEPS:
+                stage_mix(n)
+                stage_regroup(n)
+            if 1 <= n <= N_STEPS:
+                stage_sigmoid(n - 1)
+            if n % 4 == 2 and n // 4 + 1 < B:
+                prepare_vht(n // 4 + 1)
+            if n < N_STEPS:
+                stage_gate(n)
+            if 1 <= n <= N_STEPS:
+                stage_mx(n - 1)
+            if n >= 2:
+                stage_blend(n - 2)

@@ -18,22 +18,19 @@ FLOPS = 2 * B * T * C * CO + 2 * B * T * DV * CO
 N_STEPS = 4 * B
 L_ORDER = (3, 0, 1, 2)
 NG = 128
-X_AHEAD = 5
-
-
-def planes():
-    return [(g, u, e) for g in range(2) for u in range(2) for e in range(2)]
+X_AHEAD = 4
 
 
 def tile_full_tmix_params_pb_t_kernel(tc, x, x_v, W_v, v_hid, v2, v0, v_first, out):
     nc = tc.nc
     with ExitStack() as ctx:
         const = ctx.enter_context(tc.tile_pool(name="const", bufs=1))
-        xin = ctx.enter_context(tc.tile_pool(name="xin", bufs=X_AHEAD + 1))
+        xin = ctx.enter_context(tc.tile_pool(name="xin", bufs=X_AHEAD + 2))
         seqp = ctx.enter_context(tc.tile_pool(name="seqp", bufs=3))
         work = ctx.enter_context(tc.tile_pool(name="work", bufs=3))
         ep = ctx.enter_context(tc.tile_pool(name="ep", bufs=3))
         psum = ctx.enter_context(tc.psum_pool(name="psum", bufs=1))
+        ctx.enter_context(tc.manual_schedule())
 
         def l_key(k):
             return (k // 4, L_ORDER[k % 4])
@@ -56,6 +53,184 @@ def tile_full_tmix_params_pb_t_kernel(tc, x, x_v, W_v, v_hid, v2, v0, v_first, o
             nc.sync.dma_start(out=vf[:], in_=v_first[b].rearrange("(p j) c -> p j c", j=8))
             seq_tiles[b] = (vh, vf)
 
+        banks = {}
+        a_tiles = {}
+
+        def transpose_x(k, g):
+            xw = x_tiles[k][:].bitcast(F32)
+            bk = psum.tile([P, 2, 2, P], F32, tag="xt", bufs=4, name="xt_ps")
+            for u in range(2):
+                for i in range(2):
+                    c0 = (2 * g + u) * P
+                    nc.tensor.transpose(bk[:, u, i, :], xw[:, i, c0 : c0 + P], ident_f[:])
+            banks[(l_key(k), g)] = bk[:].bitcast(BF16).rearrange("p u i (r e) -> p u i r e", e=2)
+
+        def scale_x(k, g):
+            key = l_key(k)
+            if g == 0:
+                if key[1] == 3:
+                    a_tiles[key] = work.tile([P, 8, 2, P], F32, tag="a3", bufs=2, name="a3")
+                else:
+                    a_tiles[key] = work.tile([P, 8, 2, P], F32, tag="a", bufs=3, name="a")
+            a = a_tiles[key]
+            bv = banks[(key, g)]
+            for u in range(2):
+                for e in range(2):
+                    pl = 4 * g + 2 * u + e
+                    nc.scalar.activation(
+                        out=a[:, pl, :, :], in_=bv[:, u, :, :, e], func=ACT.Copy,
+                        scale=om[:, pl : pl + 1],
+                    )
+
+        xvp_tiles = {}
+
+        def mix(n, g):
+            b, s = n // 4, n % 4
+            prev = banks[((b, (s + 3) % 4), g)]
+            a = a_tiles[(b, s)]
+            if g == 0:
+                xvp_tiles[n] = work.tile([P, 8, 2, P], BF16, name="xvp")
+            xvp = xvp_tiles[n]
+            for u in range(2):
+                for e in range(2):
+                    pl = 4 * g + 2 * u + e
+                    sc = m[:, pl : pl + 1]
+                    if s > 0:
+                        nc.vector.scalar_tensor_tensor(
+                            out=xvp[:, pl, :, :], in0=prev[:, u, :, :, e], scalar=sc,
+                            in1=a[:, pl, :, :], op0=ALU.mult, op1=ALU.add,
+                        )
+                    else:
+                        nc.vector.scalar_tensor_tensor(
+                            out=xvp[:, pl, 0, 1:P], in0=prev[:, u, 1, 0 : P - 1, e], scalar=sc,
+                            in1=a[:, pl, 0, 1:P], op0=ALU.mult, op1=ALU.add,
+                        )
+                        nc.vector.scalar_tensor_tensor(
+                            out=xvp[:, pl, 1, :], in0=prev[:, u, 0, :, e], scalar=sc,
+                            in1=a[:, pl, 1, :], op0=ALU.mult, op1=ALU.add,
+                        )
+            if s == 0:
+                nc.vector.tensor_copy(
+                    out=xvp[:, 4 * g : 4 * g + 4, 0, 0:1], in_=a[:, 4 * g : 4 * g + 4, 0, 0:1]
+                )
+
+        grp_tiles = {}
+
+        def regroup_pool(n, g, lo, hi):
+            if g == 0:
+                grp_tiles[n] = work.tile([P, 2, 2 * P, 4], BF16, name="grp", align_bytes=64)
+            src = xvp_tiles[n][:].rearrange("p (g t) i r -> p g (i r) t", g=2)
+            nc.gpsimd.tensor_scalar(
+                out=grp_tiles[n][:, g, lo:hi, :], in0=src[:, g, lo:hi, :], scalar1=1.0, scalar2=0.0,
+                op0=ALU.mult, op1=ALU.add,
+            )
+
+        def regroup_act(n, g, lo, hi):
+            src = xvp_tiles[n][:].rearrange("p (g t) i r -> p g (i r) t", g=2)
+            nc.scalar.copy(out=grp_tiles[n][:, g, lo:hi, :], in_=src[:, g, lo:hi, :])
+
+        g_tiles = {}
+
+        def gate(n):
+            b, s = n // 4, n % 4
+            vht = vht_tiles[b]
+            g_ps = psum.tile([P, 2, CO], F32, tag="g", bufs=1, name="g_ps")
+            on_pe = n % 2 == 0
+            for i in range(2):
+                if on_pe:
+                    nc.tensor.matmul(out=g_ps[:, i, :], lhsT=ones[:], rhs=v0_row[:], start=True, stop=False)
+                nc.tensor.matmul(
+                    out=g_ps[:, i, :], lhsT=vht[:, 4 * i + s, :], rhs=v2_sb[:],
+                    start=not on_pe, stop=True,
+                )
+            g_tiles[n] = g_ps
+
+        u_tiles = {}
+
+        def add_bias(n):
+            if n % 2 == 1:
+                u_sb = ep.tile([P, 2, CO], F32, name="u_sb")
+                nc.vector.tensor_tensor(
+                    out=u_sb[:], in0=g_tiles[n][:],
+                    in1=v0_b[:].unsqueeze(1).to_broadcast([P, 2, CO]), op=ALU.add,
+                )
+                u_tiles[n] = u_sb
+
+        mix_tiles = {}
+
+        def sigmoid(n):
+            gate_in = g_tiles[n] if n % 2 == 0 else u_tiles[n]
+            mx_t = ep.tile([P, 2, CO], F32, name="mix_sb")
+            nc.scalar.activation(out=mx_t[:], in_=gate_in[:], func=ACT.Sigmoid)
+            mix_tiles[n] = mx_t
+
+        q_tiles = {}
+
+        def quantise(n):
+            xc = work.tile([P, 4 * P], U32, name="xc", align_bytes=64)
+            xs = work.tile([P, 4 * P], U8, name="xs", align_bytes=64)
+            nc.vector.quantize_mx(
+                out=xc[:].bitcast(FP8X4), scales=xs[:],
+                in_=grp_tiles[n][:].rearrange("p g n t -> p (g n t)"),
+            )
+            q_tiles[n] = (xc, xs)
+
+        v_tiles = {}
+
+        def project(n):
+            xc, xs = q_tiles[n]
+            v_ps = psum.tile([P, 2, CO], F32, tag="v", bufs=2, name="v_ps")
+            for i in range(2):
+                for g in range(2):
+                    c0 = g * 2 * P + i * P
+                    nc.tensor.matmul_mx(
+                        out=v_ps[:, i, :],
+                        lhsT=xc[:, c0 : c0 + P].bitcast(FP8X4),
+                        lhsT_scale=xs[:, c0 : c0 + P],
+                        rhs=w_codes[:, g * CO : (g + 1) * CO].bitcast(FP8X4),
+                        rhs_scale=w_scales[:, g * CO : (g + 1) * CO],
+                        start=(g == 0),
+                        stop=(g == 1),
+                    )
+            v_tiles[n] = v_ps
+
+        e_tiles = {}
+        f_tiles = {}
+
+        def blend_sub(n):
+            b, s = n // 4, n % 4
+            vf = seq_tiles[b][1][:].rearrange("p (i s) c -> p i s c", s=4)[:, :, s, :]
+            e_sb = ep.tile([P, 2, CO], F32, name="e_sb")
+            nc.vector.tensor_tensor(out=e_sb[:], in0=vf, in1=v_tiles[n][:], op=ALU.subtract)
+            e_tiles[n] = e_sb
+
+        def blend_mul(n):
+            f_sb = ep.tile([P, 2, CO], F32, name="f_sb")
+            nc.gpsimd.tensor_tensor(out=f_sb[:], in0=e_tiles[n][:], in1=mix_tiles[n][:], op=ALU.mult)
+            f_tiles[n] = f_sb
+
+        def blend_add(n):
+            b, s = n // 4, n % 4
+            o_sb = ep.tile([P, 2, CO], F32, name="o_sb")
+            nc.vector.tensor_tensor(out=o_sb[:], in0=f_tiles[n][:], in1=v_tiles[n][:], op=ALU.add)
+            dst = out[b].rearrange("(p i s) c -> p i s c", i=2, s=4)
+            nc.sync.dma_start(out=dst[:, :, s, :], in_=o_sb[:])
+
+        vht_tiles = {}
+        vh_banks = {}
+
+        def transpose_vh(b):
+            vh = seq_tiles[b][0]
+            vh_ps = psum.tile([P, 8, P], BF16, tag="st", bufs=1, name="vh_ps")
+            for j in range(8):
+                nc.tensor.transpose(vh_ps[:, j, :], vh[:, j, :], ident_b[:])
+            vh_banks[b] = vh_ps
+
+        def copy_vh(b):
+            vht = seqp.tile([P, 8, P], BF16, name="vht")
+            nc.scalar.copy(out=vht[:], in_=vh_banks[b][:])
+            vht_tiles[b] = vht
+
         xv_rows = const.tile([P, P], F32, name="xv_rows")
         nc.vector.memset(xv_rows[:], 0.0)
         nc.sync.dma_start(
@@ -72,7 +247,7 @@ def tile_full_tmix_params_pb_t_kernel(tc, x, x_v, W_v, v_hid, v2, v0, v_first, o
         v2_sb = const.tile([P, CO], BF16, name="v2_sb")
         nc.sync.dma_start(out=v2_sb[:], in_=v2)
         load_seq(0)
-        for k in range(2, X_AHEAD):
+        for k in range(2, X_AHEAD + 2):
             load_x(k)
 
         ident_f = const.tile([P, P], F32, name="ident_f")
@@ -82,222 +257,84 @@ def tile_full_tmix_params_pb_t_kernel(tc, x, x_v, W_v, v_hid, v2, v0, v_first, o
         ones = const.tile([P, P], BF16, name="ones")
         nc.vector.memset(ones[:], 1.0)
 
-        xv_ps = psum.tile([P, 2, 2, P], F32, tag="xt", bufs=4, name="xv_ps")
-        nc.tensor.transpose(xv_ps[:, 0, 0, :], xv_rows[:], ident_f[:])
+        xv_ps = psum.tile([P, P], F32, tag="st", bufs=1, name="xv_ps")
+        nc.tensor.transpose(xv_ps[:], xv_rows[:], ident_f[:])
         m = const.tile([P, 8], F32, name="m")
-        nc.vector.tensor_copy(out=m[:], in_=xv_ps[:, 0, 0, 0:4].bitcast(BF16))
+        nc.vector.tensor_copy(out=m[:], in_=xv_ps[:, 0:4].bitcast(BF16))
         om = const.tile([P, 8], F32, name="om")
         nc.vector.tensor_scalar(
             out=om[:], in0=m[:], scalar1=-1.0, scalar2=1.0, op0=ALU.mult, op1=ALU.add
         )
-
-        def prepare_w():
-            w_words = w_sb[:].bitcast(F32)
-            w_grp = const.tile([P, 2, CO, 4], BF16, name="w_grp", align_bytes=64)
-            w_grp_words = w_grp[:].bitcast(F32)
+        for k in range(2):
             for g in range(2):
-                w_ps = psum.tile([P, 2, 2, P], F32, tag="xt", bufs=4, name="w_ps")
-                for u in range(2):
-                    for h in range(2):
-                        c0 = (2 * g + u) * P
-                        nc.tensor.transpose(w_ps[:, u, h, :], w_words[:, h, c0 : c0 + P], ident_f[:])
-                nc.vector.tensor_copy(
-                    out=w_grp_words[:, g, :, :], in_=w_ps[:].rearrange("p u h r -> p (h r) u")
-                )
-            w_codes = const.tile([P, 2 * CO], U32, name="w_codes", align_bytes=64)
-            w_scales = const.tile([P, 2 * CO], U8, name="w_scales", align_bytes=64)
-            nc.vector.quantize_mx(
-                out=w_codes[:].bitcast(FP8X4),
-                scales=w_scales[:],
-                in_=w_grp[:].rearrange("p g c t -> p (g c t)"),
+                transpose_x(k, g)
+                scale_x(k, g)
+
+        w_words = w_sb[:].bitcast(F32)
+        w_grp = const.tile([P, 2, CO, 4], BF16, name="w_grp", align_bytes=64)
+        w_grp_words = w_grp[:].bitcast(F32)
+        for g in range(2):
+            w_ps = psum.tile([P, 2, 2, P], F32, tag="v", bufs=2, name="w_ps")
+            for u in range(2):
+                for h in range(2):
+                    c0 = (2 * g + u) * P
+                    nc.tensor.transpose(w_ps[:, u, h, :], w_words[:, h, c0 : c0 + P], ident_f[:])
+            nc.vector.tensor_copy(
+                out=w_grp_words[:, g, :, :], in_=w_ps[:].rearrange("p u h r -> p (h r) u")
             )
-            return w_codes, w_scales
+        w_codes = const.tile([P, 2 * CO], U32, name="w_codes", align_bytes=64)
+        w_scales = const.tile([P, 2 * CO], U8, name="w_scales", align_bytes=64)
+        nc.vector.quantize_mx(
+            out=w_codes[:].bitcast(FP8X4), scales=w_scales[:],
+            in_=w_grp[:].rearrange("p g c t -> p (g c t)"),
+        )
+        b_ps = psum.tile([P, 2, CO], F32, tag="g", bufs=1, name="b_ps")
+        nc.tensor.matmul(out=b_ps[:, 0, :], lhsT=ones[:], rhs=v0_row[:], start=True, stop=True)
+        v0_b = const.tile([P, CO], F32, name="v0_b")
+        nc.vector.tensor_copy(out=v0_b[:], in_=b_ps[:, 0, :])
+        transpose_vh(0)
+        copy_vh(0)
 
-        def prepare_bias():
-            b_ps = psum.tile([P, 2, CO], F32, tag="g", bufs=1, name="b_ps")
-            nc.tensor.matmul(out=b_ps[:, 0, :], lhsT=ones[:], rhs=v0_row[:], start=True, stop=True)
-            v0_b = const.tile([P, CO], F32, name="v0_b")
-            nc.vector.tensor_copy(out=v0_b[:], in_=b_ps[:, 0, :])
-            return v0_b
+        def live(n):
+            return 0 <= n < N_STEPS
 
-        vht_tiles = {}
-
-        def prepare_vht(b):
-            vh = seq_tiles[b][0]
-            vh_ps = psum.tile([P, 8, P], BF16, tag="st", bufs=1, name="vh_ps")
-            for j in range(8):
-                nc.tensor.transpose(vh_ps[:, j, :], vh[:, j, :], ident_b[:])
-            vht = seqp.tile([P, 8, P], BF16, name="vht")
-            nc.scalar.copy(out=vht[:], in_=vh_ps[:])
-            vht_tiles[b] = vht
-
-        banks = {}
-        a_tiles = {}
-
-        def stage_l(k):
-            key = l_key(k)
-            xw = x_tiles[k][:].bitcast(F32)
-            if key[1] == 3:
-                a = work.tile([P, 8, 2, P], F32, tag="a3", bufs=2, name="a3")
-            else:
-                a = work.tile([P, 8, 2, P], F32, tag="a", bufs=3, name="a")
-            views = []
-            for g in range(2):
-                bk = psum.tile([P, 2, 2, P], F32, tag="xt", bufs=4, name="xt_ps")
-                for u in range(2):
-                    for i in range(2):
-                        c0 = (2 * g + u) * P
-                        nc.tensor.transpose(bk[:, u, i, :], xw[:, i, c0 : c0 + P], ident_f[:])
-                bv = bk[:].bitcast(BF16).rearrange("p u i (r e) -> p u i r e", e=2)
-                for u in range(2):
-                    for e in range(2):
-                        pl = 4 * g + 2 * u + e
-                        nc.scalar.activation(
-                            out=a[:, pl, :, :],
-                            in_=bv[:, u, :, :, e],
-                            func=ACT.Copy,
-                            scale=om[:, pl : pl + 1],
-                        )
-                views.append(bv)
-            banks[key] = views
-            a_tiles[key] = a
-
-        xvp_tiles = {}
-
-        def stage_mix(n):
-            b, s = n // 4, n % 4
-            prev = banks[(b, (s + 3) % 4)]
-            a = a_tiles[(b, s)]
-            xvp = work.tile([P, 8, 2, P], BF16, name="xvp")
-            for g, u, e in planes():
-                pl = 4 * g + 2 * u + e
-                sc = m[:, pl : pl + 1]
-                if s > 0:
-                    nc.vector.scalar_tensor_tensor(
-                        out=xvp[:, pl, :, :], in0=prev[g][:, u, :, :, e], scalar=sc,
-                        in1=a[:, pl, :, :], op0=ALU.mult, op1=ALU.add,
-                    )
-                else:
-                    nc.vector.scalar_tensor_tensor(
-                        out=xvp[:, pl, 0, 1:P], in0=prev[g][:, u, 1, 0 : P - 1, e], scalar=sc,
-                        in1=a[:, pl, 0, 1:P], op0=ALU.mult, op1=ALU.add,
-                    )
-                    nc.vector.scalar_tensor_tensor(
-                        out=xvp[:, pl, 1, :], in0=prev[g][:, u, 0, :, e], scalar=sc,
-                        in1=a[:, pl, 1, :], op0=ALU.mult, op1=ALU.add,
-                    )
-            if s == 0:
-                nc.vector.tensor_copy(out=xvp[:, :, 0, 0:1], in_=a[:, :, 0, 0:1])
-            xvp_tiles[n] = xvp
-
-        grp_tiles = {}
-
-        def stage_regroup(n):
-            xvp = xvp_tiles[n]
-            grp = work.tile([P, 2, 2 * P, 4], BF16, name="grp", align_bytes=64)
-            src = xvp[:].rearrange("p (g t) i r -> p g (i r) t", g=2)
-            nc.gpsimd.tensor_scalar(
-                out=grp[:, 0, :, :], in0=src[:, 0, :, :], scalar1=1.0, scalar2=0.0,
-                op0=ALU.mult, op1=ALU.add,
-            )
-            nc.gpsimd.tensor_scalar(
-                out=grp[:, 1, 0:NG, :], in0=src[:, 1, 0:NG, :], scalar1=1.0, scalar2=0.0,
-                op0=ALU.mult, op1=ALU.add,
-            )
-            nc.scalar.copy(out=grp[:, 1, NG:, :], in_=src[:, 1, NG:, :])
-            grp_tiles[n] = grp
-
-        g_tiles = {}
-
-        def stage_gate(n):
-            b, s = n // 4, n % 4
-            vht = vht_tiles[b]
-            g_ps = psum.tile([P, 2, CO], F32, tag="g", bufs=1, name="g_ps")
-            on_pe = n % 2 == 0
-            for i in range(2):
-                if on_pe:
-                    nc.tensor.matmul(out=g_ps[:, i, :], lhsT=ones[:], rhs=v0_row[:], start=True, stop=False)
-                nc.tensor.matmul(
-                    out=g_ps[:, i, :], lhsT=vht[:, 4 * i + s, :], rhs=v2_sb[:],
-                    start=not on_pe, stop=True,
-                )
-            g_tiles[n] = g_ps
-
-        mix_tiles = {}
-
-        def stage_sigmoid(n):
-            g_ps = g_tiles[n]
-            mix = ep.tile([P, 2, CO], F32, name="mix")
-            if n % 2 == 0:
-                nc.scalar.activation(out=mix[:], in_=g_ps[:], func=ACT.Sigmoid)
-            else:
-                u_sb = ep.tile([P, 2, CO], F32, name="u_sb")
-                nc.vector.tensor_tensor(
-                    out=u_sb[:], in0=g_ps[:], in1=v0_b[:].unsqueeze(1).to_broadcast([P, 2, CO]),
-                    op=ALU.add,
-                )
-                nc.scalar.activation(out=mix[:], in_=u_sb[:], func=ACT.Sigmoid)
-            mix_tiles[n] = mix
-
-        v_tiles = {}
-
-        def stage_mx(n):
-            grp = grp_tiles[n]
-            xc = work.tile([P, 4 * P], U32, name="xc", align_bytes=64)
-            xs = work.tile([P, 4 * P], U8, name="xs", align_bytes=64)
-            nc.vector.quantize_mx(
-                out=xc[:].bitcast(FP8X4), scales=xs[:], in_=grp[:].rearrange("p g n t -> p (g n t)")
-            )
-            v_ps = psum.tile([P, 2, CO], F32, tag="v", bufs=2, name="v_ps")
-            for i in range(2):
-                for g in range(2):
-                    c0 = g * 2 * P + i * P
-                    nc.tensor.matmul_mx(
-                        out=v_ps[:, i, :],
-                        lhsT=xc[:, c0 : c0 + P].bitcast(FP8X4),
-                        lhsT_scale=xs[:, c0 : c0 + P],
-                        rhs=w_codes[:, g * CO : (g + 1) * CO].bitcast(FP8X4),
-                        rhs_scale=w_scales[:, g * CO : (g + 1) * CO],
-                        start=(g == 0),
-                        stop=(g == 1),
-                    )
-            v_tiles[n] = v_ps
-
-        def stage_blend(n):
-            b, s = n // 4, n % 4
-            v_ps = v_tiles[n]
-            mix = mix_tiles[n]
-            vf = seq_tiles[b][1][:].rearrange("p (i s) c -> p i s c", s=4)[:, :, s, :]
-            e_sb = ep.tile([P, 2, CO], F32, name="e_sb")
-            nc.vector.tensor_tensor(out=e_sb[:], in0=vf, in1=v_ps[:], op=ALU.subtract)
-            f_sb = ep.tile([P, 2, CO], F32, name="f_sb")
-            nc.gpsimd.tensor_tensor(out=f_sb[:], in0=e_sb[:], in1=mix[:], op=ALU.mult)
-            o_sb = ep.tile([P, 2, CO], F32, name="o_sb")
-            nc.vector.tensor_tensor(out=o_sb[:], in0=f_sb[:], in1=v_ps[:], op=ALU.add)
-            dst = out[b].rearrange("(p i s) c -> p i s c", i=2, s=4)
-            nc.sync.dma_start(out=dst[:, :, s, :], in_=o_sb[:])
-
-        stage_l(0)
-        w_codes, w_scales = prepare_w()
-        v0_b = prepare_bias()
-        prepare_vht(0)
-        for n in range(N_STEPS + 2):
-            if n + X_AHEAD < N_STEPS:
-                load_x(n + X_AHEAD)
+        for n in range(N_STEPS + 3):
+            if n + X_AHEAD + 2 < N_STEPS:
+                load_x(n + X_AHEAD + 2)
             if n % 4 == 0 and n // 4 + 1 < B:
                 load_seq(n // 4 + 1)
-            if n + 1 < N_STEPS:
-                stage_l(n + 1)
-            if n < N_STEPS:
-                stage_mix(n)
-                stage_regroup(n)
-            if 1 <= n <= N_STEPS:
-                stage_sigmoid(n - 1)
+            if live(n):
+                mix(n, 0)
+            if live(n + 2):
+                transpose_x(n + 2, 0)
+            if live(n - 3):
+                blend_add(n - 3)
+            if live(n - 2):
+                blend_sub(n - 2)
+            if live(n):
+                regroup_pool(n, 0, 0, 2 * P)
+            if live(n - 2):
+                blend_mul(n - 2)
+            if live(n + 2):
+                scale_x(n + 2, 0)
+            if live(n - 1):
+                gate(n - 1)
+            if live(n):
+                mix(n, 1)
+            if live(n + 2):
+                transpose_x(n + 2, 1)
+            if live(n):
+                regroup_act(n, 1, NG, 2 * P)
+            if live(n - 1):
+                quantise(n - 1)
+                project(n - 1)
+            if live(n + 2):
+                scale_x(n + 2, 1)
+            if live(n):
+                regroup_pool(n, 1, 0, NG)
+            if live(n - 1):
+                add_bias(n - 1)
+                sigmoid(n - 1)
             if n % 4 == 2 and n // 4 + 1 < B:
-                prepare_vht(n // 4 + 1)
-            if n < N_STEPS:
-                stage_gate(n)
-            if 1 <= n <= N_STEPS:
-                stage_mx(n - 1)
-            if n >= 2:
-                stage_blend(n - 2)
+                transpose_vh(n // 4 + 1)
+                copy_vh(n // 4 + 1)

@@ -17,7 +17,7 @@ FLOPS = 2 * B * T * C * CO + 2 * B * T * DV * CO
 
 N_STEPS = 4 * B
 L_ORDER = (3, 0, 1, 2)
-NG = 128
+NG1 = 64
 X_AHEAD = 4
 
 
@@ -118,16 +118,21 @@ def tile_full_tmix_params_pb_t_kernel(tc, x, x_v, W_v, v_hid, v2, v0, v_first, o
 
         def regroup_pool(n, g, lo, hi):
             if g == 0:
-                grp_tiles[n] = work.tile([P, 2, 2 * P, 4], BF16, name="grp", align_bytes=64)
+                grp_tiles[(n, g)] = work.tile([P, 2 * P, 4], BF16, tag="grp0", bufs=1, name="grp0", align_bytes=64)
+            else:
+                grp_tiles[(n, g)] = work.tile([P, 2 * P, 4], BF16, tag="grp1", bufs=2, name="grp1", align_bytes=64)
             src = xvp_tiles[n][:].rearrange("p (g t) i r -> p g (i r) t", g=2)
             nc.gpsimd.tensor_scalar(
-                out=grp_tiles[n][:, g, lo:hi, :], in0=src[:, g, lo:hi, :], scalar1=1.0, scalar2=0.0,
+                out=grp_tiles[(n, g)][:, lo:hi, :], in0=src[:, g, lo:hi, :], scalar1=1.0, scalar2=0.0,
                 op0=ALU.mult, op1=ALU.add,
             )
 
         def regroup_act(n, g, lo, hi):
-            src = xvp_tiles[n][:].rearrange("p (g t) i r -> p g (i r) t", g=2)
-            nc.scalar.copy(out=grp_tiles[n][:, g, lo:hi, :], in_=src[:, g, lo:hi, :])
+            src = xvp_tiles[n][:].rearrange("p (g t) i r -> p g t (i r)", g=2)
+            nc.scalar.copy(
+                out=grp_tiles[(n, g)][:, lo:hi, :].rearrange("p (c i) t -> p c t i", i=4),
+                in_=src[:, g, :, lo:hi].rearrange("p t (c i) -> p c t i", i=4),
+            )
 
         g_tiles = {}
 
@@ -169,10 +174,12 @@ def tile_full_tmix_params_pb_t_kernel(tc, x, x_v, W_v, v_hid, v2, v0, v_first, o
         def quantise(n):
             xc = work.tile([P, 4 * P], U32, name="xc", align_bytes=64)
             xs = work.tile([P, 4 * P], U8, name="xs", align_bytes=64)
-            nc.vector.quantize_mx(
-                out=xc[:].bitcast(FP8X4), scales=xs[:],
-                in_=grp_tiles[n][:].rearrange("p g n t -> p (g n t)"),
-            )
+            for g in range(2):
+                nc.vector.quantize_mx(
+                    out=xc[:, g * 2 * P : (g + 1) * 2 * P].bitcast(FP8X4),
+                    scales=xs[:, g * 2 * P : (g + 1) * 2 * P],
+                    in_=grp_tiles[(n, g)][:].rearrange("p n t -> p (n t)"),
+                )
             q_tiles[n] = (xc, xs)
 
         v_tiles = {}
@@ -249,6 +256,7 @@ def tile_full_tmix_params_pb_t_kernel(tc, x, x_v, W_v, v_hid, v2, v0, v_first, o
         load_seq(0)
         for k in range(2, X_AHEAD + 2):
             load_x(k)
+        load_seq(1)
 
         ident_f = const.tile([P, P], F32, name="ident_f")
         make_identity(nc, ident_f[:])
@@ -265,10 +273,10 @@ def tile_full_tmix_params_pb_t_kernel(tc, x, x_v, W_v, v_hid, v2, v0, v_first, o
         nc.vector.tensor_scalar(
             out=om[:], in0=m[:], scalar1=-1.0, scalar2=1.0, op0=ALU.mult, op1=ALU.add
         )
-        for k in range(2):
-            for g in range(2):
-                transpose_x(k, g)
-                scale_x(k, g)
+        for k, g in ((0, 0), (0, 1), (1, 0)):
+            transpose_x(k, g)
+            scale_x(k, g)
+        transpose_x(1, 1)
 
         w_words = w_sb[:].bitcast(F32)
         w_grp = const.tile([P, 2, CO, 4], BF16, name="w_grp", align_bytes=64)
@@ -301,40 +309,41 @@ def tile_full_tmix_params_pb_t_kernel(tc, x, x_v, W_v, v_hid, v2, v0, v_first, o
         for n in range(N_STEPS + 3):
             if n + X_AHEAD + 2 < N_STEPS:
                 load_x(n + X_AHEAD + 2)
-            if n % 4 == 0 and n // 4 + 1 < B:
-                load_seq(n // 4 + 1)
+            if n % 4 == 2 and n // 4 + 2 < B:
+                load_seq(n // 4 + 2)
             if live(n):
                 mix(n, 0)
+            if live(n - 1):
+                regroup_act(n - 1, 1, NG1, 2 * P)
+                add_bias(n - 1)
             if live(n + 2):
                 transpose_x(n + 2, 0)
+            if live(n + 1):
+                scale_x(n + 1, 1)
             if live(n - 3):
                 blend_add(n - 3)
+            if live(n - 1):
+                quantise(n - 1)
+                project(n - 1)
+            if live(n):
+                regroup_pool(n, 0, 0, 2 * P)
+            if live(n - 1):
+                sigmoid(n - 1)
             if live(n - 2):
                 blend_sub(n - 2)
             if live(n):
-                regroup_pool(n, 0, 0, 2 * P)
+                gate(n)
+            if n % 4 == 1 and n // 4 + 1 < B:
+                transpose_vh(n // 4 + 1)
             if live(n - 2):
                 blend_mul(n - 2)
             if live(n + 2):
                 scale_x(n + 2, 0)
-            if live(n - 1):
-                gate(n - 1)
+            if n % 4 == 1 and n // 4 + 1 < B:
+                copy_vh(n // 4 + 1)
             if live(n):
                 mix(n, 1)
             if live(n + 2):
                 transpose_x(n + 2, 1)
             if live(n):
-                regroup_act(n, 1, NG, 2 * P)
-            if live(n - 1):
-                quantise(n - 1)
-                project(n - 1)
-            if live(n + 2):
-                scale_x(n + 2, 1)
-            if live(n):
-                regroup_pool(n, 1, 0, NG)
-            if live(n - 1):
-                add_bias(n - 1)
-                sigmoid(n - 1)
-            if n % 4 == 2 and n // 4 + 1 < B:
-                transpose_vh(n // 4 + 1)
-                copy_vh(n // 4 + 1)
+                regroup_pool(n, 1, 0, NG1)

@@ -316,10 +316,18 @@ def tile_full_tmix_params_pb_t_kernel(tc, x, x_v, W_v, v_hid, v2, v0, v_first, o
             if live(n - 1):
                 regroup_act(n - 1, 1, NG1, 2 * P)
                 add_bias(n - 1)
+                if (n - 1) % 2 == 0:
+                    sigmoid(n - 1)
             if live(n + 2):
                 transpose_x(n + 2, 0)
+            if live(n):
+                gate(n)
+            if n % 4 == 1 and n // 4 + 1 < B:
+                transpose_vh(n // 4 + 1)
             if live(n + 1):
                 scale_x(n + 1, 1)
+            if live(n - 1) and (n - 1) % 2 == 1:
+                sigmoid(n - 1)
             if live(n - 3):
                 blend_add(n - 3)
             if live(n - 1):
@@ -327,15 +335,8 @@ def tile_full_tmix_params_pb_t_kernel(tc, x, x_v, W_v, v_hid, v2, v0, v_first, o
                 project(n - 1)
             if live(n):
                 regroup_pool(n, 0, 0, 2 * P)
-            if live(n - 1):
-                sigmoid(n - 1)
             if live(n - 2):
                 blend_sub(n - 2)
-            if live(n):
-                gate(n)
-            if n % 4 == 1 and n // 4 + 1 < B:
-                transpose_vh(n // 4 + 1)
-            if live(n - 2):
                 blend_mul(n - 2)
             if live(n + 2):
                 scale_x(n + 2, 0)

@@ -16,33 +16,33 @@ B, T, C, CO, DV = 8, 1024, 1024, 256, 128
 FLOPS = 2 * B * T * C * CO + 2 * B * T * DV * CO
 
 N_STEPS = 4 * B
-L_ORDER = (3, 0, 1, 2)
 NG1 = 64
-X_AHEAD = 4
+X_AHEAD = 6
+LOAD_ORDER = (3, 0, 1, 2)
 
 
 def tile_full_tmix_params_pb_t_kernel(tc, x, x_v, W_v, v_hid, v2, v0, v_first, out):
     nc = tc.nc
     with ExitStack() as ctx:
         const = ctx.enter_context(tc.tile_pool(name="const", bufs=1))
-        xin = ctx.enter_context(tc.tile_pool(name="xin", bufs=X_AHEAD + 2))
+        xin = ctx.enter_context(tc.tile_pool(name="xin", bufs=1))
         seqp = ctx.enter_context(tc.tile_pool(name="seqp", bufs=3))
         work = ctx.enter_context(tc.tile_pool(name="work", bufs=3))
         ep = ctx.enter_context(tc.tile_pool(name="ep", bufs=3))
         psum = ctx.enter_context(tc.psum_pool(name="psum", bufs=1))
         ctx.enter_context(tc.manual_schedule())
 
-        def l_key(k):
-            return (k // 4, L_ORDER[k % 4])
-
         x_tiles = {}
 
         def load_x(k):
-            b, s = l_key(k)
-            x_sb = xin.tile([P, 2, C], BF16, name="x_sb")
+            b, s = k // 4, LOAD_ORDER[k % 4]
+            if s == 3:
+                x_sb = xin.tile([P, 2, C], BF16, tag="x3", bufs=3, name="x3_sb")
+            else:
+                x_sb = xin.tile([P, 2, C], BF16, tag="x", bufs=6, name="x_sb")
             src = x[b].rearrange("(p i s) c -> p i s c", i=2, s=4)
             nc.sync.dma_start(out=x_sb[:], in_=src[:, :, s, :])
-            x_tiles[k] = x_sb
+            x_tiles[(b, s)] = x_sb
 
         seq_tiles = {}
 
@@ -56,24 +56,40 @@ def tile_full_tmix_params_pb_t_kernel(tc, x, x_v, W_v, v_hid, v2, v0, v_first, o
         banks = {}
         a_tiles = {}
 
-        def transpose_x(k, g):
-            xw = x_tiles[k][:].bitcast(F32)
-            bk = psum.tile([P, 2, 2, P], F32, tag="xt", bufs=4, name="xt_ps")
+        def bank_tile(g):
+            if g == 0:
+                return psum.tile([P, 2, 2, P], F32, tag="xt0", bufs=2, name="xt0_ps")
+            return psum.tile([P, 2, 2, P], F32, tag="xt1", bufs=2, name="xt1_ps")
+
+        def as_planes(bk):
+            return bk[:].bitcast(BF16).rearrange("p u i (r e) -> p u i r e", e=2)
+
+        def transpose_x(b, s, g):
+            xw = x_tiles[(b, s)][:].bitcast(F32)
+            bk = bank_tile(g)
             for u in range(2):
                 for i in range(2):
                     c0 = (2 * g + u) * P
                     nc.tensor.transpose(bk[:, u, i, :], xw[:, i, c0 : c0 + P], ident_f[:])
-            banks[(l_key(k), g)] = bk[:].bitcast(BF16).rearrange("p u i (r e) -> p u i r e", e=2)
+            banks[(b, s, g)] = as_planes(bk)
 
-        def scale_x(k, g):
-            key = l_key(k)
+        def transpose_wrap(b, g):
+            xw = x_tiles[(b, 3)][:].bitcast(F32)
+            bk = bank_tile(g)
+            for u in range(2):
+                c0 = (2 * g + u) * P
+                row = bk[:, u, :, :].rearrange("p i r -> p (i r)")
+                nc.tensor.transpose(row[:, 0:P], zeros_f[:], ident_f[:])
+                nc.tensor.transpose(row[:, 1 : P + 1], xw[:, 1, c0 : c0 + P], ident_f[:])
+                nc.tensor.transpose(row[:, P : 2 * P], xw[:, 0, c0 : c0 + P], ident_f[:])
+            banks[(b, -1, g)] = as_planes(bk)
+
+        def scale_x(n, g):
+            key = (n // 4, n % 4)
             if g == 0:
-                if key[1] == 3:
-                    a_tiles[key] = work.tile([P, 8, 2, P], F32, tag="a3", bufs=2, name="a3")
-                else:
-                    a_tiles[key] = work.tile([P, 8, 2, P], F32, tag="a", bufs=3, name="a")
+                a_tiles[key] = work.tile([P, 8, 2, P], F32, name="a")
             a = a_tiles[key]
-            bv = banks[(key, g)]
+            bv = banks[(key[0], key[1], g)]
             for u in range(2):
                 for e in range(2):
                     pl = 4 * g + 2 * u + e
@@ -86,7 +102,7 @@ def tile_full_tmix_params_pb_t_kernel(tc, x, x_v, W_v, v_hid, v2, v0, v_first, o
 
         def mix(n, g):
             b, s = n // 4, n % 4
-            prev = banks[((b, (s + 3) % 4), g)]
+            prev = banks[(b, s - 1, g)]
             a = a_tiles[(b, s)]
             if g == 0:
                 xvp_tiles[n] = work.tile([P, 8, 2, P], BF16, name="xvp")
@@ -94,43 +110,26 @@ def tile_full_tmix_params_pb_t_kernel(tc, x, x_v, W_v, v_hid, v2, v0, v_first, o
             for u in range(2):
                 for e in range(2):
                     pl = 4 * g + 2 * u + e
-                    sc = m[:, pl : pl + 1]
-                    if s > 0:
-                        nc.vector.scalar_tensor_tensor(
-                            out=xvp[:, pl, :, :], in0=prev[:, u, :, :, e], scalar=sc,
-                            in1=a[:, pl, :, :], op0=ALU.mult, op1=ALU.add,
-                        )
-                    else:
-                        nc.vector.scalar_tensor_tensor(
-                            out=xvp[:, pl, 0, 1:P], in0=prev[:, u, 1, 0 : P - 1, e], scalar=sc,
-                            in1=a[:, pl, 0, 1:P], op0=ALU.mult, op1=ALU.add,
-                        )
-                        nc.vector.scalar_tensor_tensor(
-                            out=xvp[:, pl, 1, :], in0=prev[:, u, 0, :, e], scalar=sc,
-                            in1=a[:, pl, 1, :], op0=ALU.mult, op1=ALU.add,
-                        )
-            if s == 0:
-                nc.vector.tensor_copy(
-                    out=xvp[:, 4 * g : 4 * g + 4, 0, 0:1], in_=a[:, 4 * g : 4 * g + 4, 0, 0:1]
-                )
+                    nc.vector.scalar_tensor_tensor(
+                        out=xvp[:, pl, :, :], in0=prev[:, u, :, :, e], scalar=m[:, pl : pl + 1],
+                        in1=a[:, pl, :, :], op0=ALU.mult, op1=ALU.add,
+                    )
 
         grp_tiles = {}
 
         def regroup_pool(n, g, lo, hi):
             if g == 0:
-                grp_tiles[(n, g)] = work.tile([P, 2 * P, 4], BF16, tag="grp0", bufs=1, name="grp0", align_bytes=64)
-            else:
-                grp_tiles[(n, g)] = work.tile([P, 2 * P, 4], BF16, tag="grp1", bufs=2, name="grp1", align_bytes=64)
+                grp_tiles[n] = work.tile([P, 2, 2 * P, 4], BF16, tag="grp", bufs=1, name="grp", align_bytes=64)
             src = xvp_tiles[n][:].rearrange("p (g t) i r -> p g (i r) t", g=2)
             nc.gpsimd.tensor_scalar(
-                out=grp_tiles[(n, g)][:, lo:hi, :], in0=src[:, g, lo:hi, :], scalar1=1.0, scalar2=0.0,
+                out=grp_tiles[n][:, g, lo:hi, :], in0=src[:, g, lo:hi, :], scalar1=1.0, scalar2=0.0,
                 op0=ALU.mult, op1=ALU.add,
             )
 
         def regroup_act(n, g, lo, hi):
             src = xvp_tiles[n][:].rearrange("p (g t) i r -> p g t (i r)", g=2)
             nc.scalar.copy(
-                out=grp_tiles[(n, g)][:, lo:hi, :].rearrange("p (c i) t -> p c t i", i=4),
+                out=grp_tiles[n][:, g, lo:hi, :].rearrange("p (c i) t -> p c t i", i=4),
                 in_=src[:, g, :, lo:hi].rearrange("p t (c i) -> p c t i", i=4),
             )
 
@@ -140,33 +139,22 @@ def tile_full_tmix_params_pb_t_kernel(tc, x, x_v, W_v, v_hid, v2, v0, v_first, o
             b, s = n // 4, n % 4
             vht = vht_tiles[b]
             g_ps = psum.tile([P, 2, CO], F32, tag="g", bufs=1, name="g_ps")
-            on_pe = n % 2 == 0
             for i in range(2):
-                if on_pe:
-                    nc.tensor.matmul(out=g_ps[:, i, :], lhsT=ones[:], rhs=v0_row[:], start=True, stop=False)
+                for h in range(2):
+                    nc.tensor.matmul(
+                        out=g_ps[:, i, h * P : (h + 1) * P], lhsT=v0_wide[:, h, :], rhs=ident_f[:],
+                        is_transpose=True, start=(h == 0), stop=False,
+                    )
                 nc.tensor.matmul(
-                    out=g_ps[:, i, :], lhsT=vht[:, 4 * i + s, :], rhs=v2_sb[:],
-                    start=not on_pe, stop=True,
+                    out=g_ps[:, i, :], lhsT=vht[:, 4 * i + s, :], rhs=v2_sb[:], start=False, stop=True
                 )
             g_tiles[n] = g_ps
-
-        u_tiles = {}
-
-        def add_bias(n):
-            if n % 2 == 1:
-                u_sb = ep.tile([P, 2, CO], F32, name="u_sb")
-                nc.vector.tensor_tensor(
-                    out=u_sb[:], in0=g_tiles[n][:],
-                    in1=v0_b[:].unsqueeze(1).to_broadcast([P, 2, CO]), op=ALU.add,
-                )
-                u_tiles[n] = u_sb
 
         mix_tiles = {}
 
         def sigmoid(n):
-            gate_in = g_tiles[n] if n % 2 == 0 else u_tiles[n]
             mx_t = ep.tile([P, 2, CO], F32, name="mix_sb")
-            nc.scalar.activation(out=mx_t[:], in_=gate_in[:], func=ACT.Sigmoid)
+            nc.scalar.activation(out=mx_t[:], in_=g_tiles[n][:], func=ACT.Sigmoid)
             mix_tiles[n] = mx_t
 
         q_tiles = {}
@@ -174,12 +162,10 @@ def tile_full_tmix_params_pb_t_kernel(tc, x, x_v, W_v, v_hid, v2, v0, v_first, o
         def quantise(n):
             xc = work.tile([P, 4 * P], U32, name="xc", align_bytes=64)
             xs = work.tile([P, 4 * P], U8, name="xs", align_bytes=64)
-            for g in range(2):
-                nc.vector.quantize_mx(
-                    out=xc[:, g * 2 * P : (g + 1) * 2 * P].bitcast(FP8X4),
-                    scales=xs[:, g * 2 * P : (g + 1) * 2 * P],
-                    in_=grp_tiles[(n, g)][:].rearrange("p n t -> p (n t)"),
-                )
+            nc.vector.quantize_mx(
+                out=xc[:].bitcast(FP8X4), scales=xs[:],
+                in_=grp_tiles[n][:].rearrange("p g n t -> p (g n t)"),
+            )
             q_tiles[n] = (xc, xs)
 
         v_tiles = {}
@@ -213,7 +199,10 @@ def tile_full_tmix_params_pb_t_kernel(tc, x, x_v, W_v, v_hid, v2, v0, v_first, o
 
         def blend_mul(n):
             f_sb = ep.tile([P, 2, CO], F32, name="f_sb")
-            nc.gpsimd.tensor_tensor(out=f_sb[:], in0=e_tiles[n][:], in1=mix_tiles[n][:], op=ALU.mult)
+            if n < N_STEPS - 2:
+                nc.gpsimd.tensor_tensor(out=f_sb[:], in0=e_tiles[n][:], in1=mix_tiles[n][:], op=ALU.mult)
+            else:
+                nc.vector.tensor_tensor(out=f_sb[:], in0=e_tiles[n][:], in1=mix_tiles[n][:], op=ALU.mult)
             f_tiles[n] = f_sb
 
         def blend_add(n):
@@ -248,13 +237,13 @@ def tile_full_tmix_params_pb_t_kernel(tc, x, x_v, W_v, v_hid, v2, v0, v_first, o
         load_x(1)
         w_sb = const.tile([P, 2, C], BF16, name="w_sb")
         nc.sync.dma_start(out=w_sb[:], in_=W_v.rearrange("(h p) c -> p h c", p=P))
-        v0_row = const.tile([P, CO], BF16, name="v0_row")
-        nc.vector.memset(v0_row[:], 0.0)
-        nc.sync.dma_start(out=v0_row[0:1, :], in_=v0.rearrange("a b c -> (a b) c"))
+        v0_rows = const.tile([P, P], BF16, name="v0_rows")
+        nc.vector.memset(v0_rows[:], 0.0)
+        nc.sync.dma_start(out=v0_rows[0:2, :], in_=v0.rearrange("a b (h c) -> (a b h) c", h=2))
         v2_sb = const.tile([P, CO], BF16, name="v2_sb")
         nc.sync.dma_start(out=v2_sb[:], in_=v2)
         load_seq(0)
-        for k in range(2, X_AHEAD + 2):
+        for k in range(2, X_AHEAD):
             load_x(k)
         load_seq(1)
 
@@ -262,8 +251,8 @@ def tile_full_tmix_params_pb_t_kernel(tc, x, x_v, W_v, v_hid, v2, v0, v_first, o
         make_identity(nc, ident_f[:])
         ident_b = const.tile([P, P], BF16, name="ident_b")
         make_identity(nc, ident_b[:])
-        ones = const.tile([P, P], BF16, name="ones")
-        nc.vector.memset(ones[:], 1.0)
+        zeros_f = const.tile([P, P], F32, name="zeros_f")
+        nc.vector.memset(zeros_f[:], 0.0)
 
         xv_ps = psum.tile([P, P], F32, tag="st", bufs=1, name="xv_ps")
         nc.tensor.transpose(xv_ps[:], xv_rows[:], ident_f[:])
@@ -273,10 +262,18 @@ def tile_full_tmix_params_pb_t_kernel(tc, x, x_v, W_v, v_hid, v2, v0, v_first, o
         nc.vector.tensor_scalar(
             out=om[:], in0=m[:], scalar1=-1.0, scalar2=1.0, op0=ALU.mult, op1=ALU.add
         )
-        for k, g in ((0, 0), (0, 1), (1, 0)):
-            transpose_x(k, g)
-            scale_x(k, g)
-        transpose_x(1, 1)
+        transpose_wrap(0, 0)
+        transpose_x(0, 0, 0)
+        scale_x(0, 0)
+        transpose_wrap(0, 1)
+        transpose_x(0, 0, 1)
+
+        v0_ps = psum.tile([P, P], BF16, tag="st", bufs=1, name="v0_ps")
+        nc.tensor.transpose(v0_ps[:], v0_rows[:], ident_b[:])
+        v0_col = const.tile([P, 2], F32, name="v0_col")
+        nc.vector.tensor_copy(out=v0_col[:], in_=v0_ps[:, 0:2])
+        v0_wide = const.tile([P, 2, P], F32, name="v0_wide")
+        nc.vector.tensor_copy(out=v0_wide[:], in_=v0_col[:].unsqueeze(2).to_broadcast([P, 2, P]))
 
         w_words = w_sb[:].bitcast(F32)
         w_grp = const.tile([P, 2, CO, 4], BF16, name="w_grp", align_bytes=64)
@@ -296,38 +293,37 @@ def tile_full_tmix_params_pb_t_kernel(tc, x, x_v, W_v, v_hid, v2, v0, v_first, o
             out=w_codes[:].bitcast(FP8X4), scales=w_scales[:],
             in_=w_grp[:].rearrange("p g c t -> p (g c t)"),
         )
-        b_ps = psum.tile([P, 2, CO], F32, tag="g", bufs=1, name="b_ps")
-        nc.tensor.matmul(out=b_ps[:, 0, :], lhsT=ones[:], rhs=v0_row[:], start=True, stop=True)
-        v0_b = const.tile([P, CO], F32, name="v0_b")
-        nc.vector.tensor_copy(out=v0_b[:], in_=b_ps[:, 0, :])
         transpose_vh(0)
         copy_vh(0)
 
         def live(n):
             return 0 <= n < N_STEPS
 
+        def refill(n, g):
+            b, s = n // 4, n % 4
+            if s < 3:
+                transpose_x(b, s + 1, g)
+            elif b + 1 < B:
+                transpose_x(b + 1, 0, g)
+                transpose_wrap(b + 1, g)
+
         for n in range(N_STEPS + 3):
-            if n + X_AHEAD + 2 < N_STEPS:
-                load_x(n + X_AHEAD + 2)
+            if n + X_AHEAD < N_STEPS:
+                load_x(n + X_AHEAD)
             if n % 4 == 2 and n // 4 + 2 < B:
                 load_seq(n // 4 + 2)
             if live(n):
                 mix(n, 0)
             if live(n - 1):
                 regroup_act(n - 1, 1, NG1, 2 * P)
-                add_bias(n - 1)
-                if (n - 1) % 2 == 0:
-                    sigmoid(n - 1)
-            if live(n + 2):
-                transpose_x(n + 2, 0)
+                sigmoid(n - 1)
             if live(n):
+                refill(n, 0)
                 gate(n)
             if n % 4 == 1 and n // 4 + 1 < B:
                 transpose_vh(n // 4 + 1)
-            if live(n + 1):
-                scale_x(n + 1, 1)
-            if live(n - 1) and (n - 1) % 2 == 1:
-                sigmoid(n - 1)
+            if live(n):
+                scale_x(n, 1)
             if live(n - 3):
                 blend_add(n - 3)
             if live(n - 1):
@@ -338,13 +334,11 @@ def tile_full_tmix_params_pb_t_kernel(tc, x, x_v, W_v, v_hid, v2, v0, v_first, o
             if live(n - 2):
                 blend_sub(n - 2)
                 blend_mul(n - 2)
-            if live(n + 2):
-                scale_x(n + 2, 0)
+            if live(n + 1):
+                scale_x(n + 1, 0)
             if n % 4 == 1 and n // 4 + 1 < B:
                 copy_vh(n // 4 + 1)
             if live(n):
                 mix(n, 1)
-            if live(n + 2):
-                transpose_x(n + 2, 1)
-            if live(n):
+                refill(n, 1)
                 regroup_pool(n, 1, 0, NG1)

@@ -16,9 +16,8 @@ B, T, C, CO, DV = 8, 1024, 1024, 256, 128
 FLOPS = 2 * B * T * C * CO + 2 * B * T * DV * CO
 
 N_STEPS = 4 * B
-NG1 = 64
+NG1 = 96
 X_AHEAD = 6
-LOAD_ORDER = (3, 0, 1, 2)
 
 
 def tile_full_tmix_params_pb_t_kernel(tc, x, x_v, W_v, v_hid, v2, v0, v_first, out):
@@ -32,10 +31,13 @@ def tile_full_tmix_params_pb_t_kernel(tc, x, x_v, W_v, v_hid, v2, v0, v_first, o
         psum = ctx.enter_context(tc.psum_pool(name="psum", bufs=1))
         ctx.enter_context(tc.manual_schedule())
 
+        x_loads = [(0, 0), (0, 3), (0, 1), (0, 2)]
+        for b in range(1, B):
+            x_loads.extend([(b, 3), (b, 0), (b, 1), (b, 2)])
         x_tiles = {}
 
         def load_x(k):
-            b, s = k // 4, LOAD_ORDER[k % 4]
+            b, s = x_loads[k]
             if s == 3:
                 x_sb = xin.tile([P, 2, C], BF16, tag="x3", bufs=3, name="x3_sb")
             else:
@@ -46,12 +48,15 @@ def tile_full_tmix_params_pb_t_kernel(tc, x, x_v, W_v, v_hid, v2, v0, v_first, o
 
         seq_tiles = {}
 
-        def load_seq(b):
+        def load_vh(b):
             vh = seqp.tile([P, 8, DV], BF16, name="vh")
             nc.sync.dma_start(out=vh[:], in_=v_hid[b].rearrange("(p j) d -> p j d", j=8))
+            seq_tiles[(b, 0)] = vh
+
+        def load_vf(b):
             vf = seqp.tile([P, 8, CO], BF16, name="vf")
             nc.sync.dma_start(out=vf[:], in_=v_first[b].rearrange("(p j) c -> p j c", j=8))
-            seq_tiles[b] = (vh, vf)
+            seq_tiles[(b, 1)] = vf
 
         banks = {}
         a_tiles = {}
@@ -192,7 +197,7 @@ def tile_full_tmix_params_pb_t_kernel(tc, x, x_v, W_v, v_hid, v2, v0, v_first, o
 
         def blend_sub(n):
             b, s = n // 4, n % 4
-            vf = seq_tiles[b][1][:].rearrange("p (i s) c -> p i s c", s=4)[:, :, s, :]
+            vf = seq_tiles[(b, 1)][:].rearrange("p (i s) c -> p i s c", s=4)[:, :, s, :]
             e_sb = ep.tile([P, 2, CO], F32, name="e_sb")
             nc.vector.tensor_tensor(out=e_sb[:], in0=vf, in1=v_tiles[n][:], op=ALU.subtract)
             e_tiles[n] = e_sb
@@ -216,7 +221,7 @@ def tile_full_tmix_params_pb_t_kernel(tc, x, x_v, W_v, v_hid, v2, v0, v_first, o
         vh_banks = {}
 
         def transpose_vh(b):
-            vh = seq_tiles[b][0]
+            vh = seq_tiles[(b, 0)]
             vh_ps = psum.tile([P, 8, P], BF16, tag="st", bufs=1, name="vh_ps")
             for j in range(8):
                 nc.tensor.transpose(vh_ps[:, j, :], vh[:, j, :], ident_b[:])
@@ -229,30 +234,33 @@ def tile_full_tmix_params_pb_t_kernel(tc, x, x_v, W_v, v_hid, v2, v0, v_first, o
 
         xv_rows = const.tile([P, P], F32, name="xv_rows")
         nc.vector.memset(xv_rows[:], 0.0)
+        v0_rows = const.tile([P, P], BF16, name="v0_rows")
+        nc.vector.memset(v0_rows[:], 0.0)
+        zeros_f = const.tile([P, P], F32, name="zeros_f")
+        nc.vector.memset(zeros_f[:], 0.0)
         nc.sync.dma_start(
             out=xv_rows[:].bitcast(BF16)[0:4, :],
             in_=x_v.rearrange("a b (r c) -> (a b r) c", r=4),
         )
-        load_x(0)
-        load_x(1)
-        w_sb = const.tile([P, 2, C], BF16, name="w_sb")
-        nc.sync.dma_start(out=w_sb[:], in_=W_v.rearrange("(h p) c -> p h c", p=P))
-        v0_rows = const.tile([P, P], BF16, name="v0_rows")
-        nc.vector.memset(v0_rows[:], 0.0)
         nc.sync.dma_start(out=v0_rows[0:2, :], in_=v0.rearrange("a b (h c) -> (a b h) c", h=2))
+        for k in range(3):
+            load_x(k)
         v2_sb = const.tile([P, CO], BF16, name="v2_sb")
         nc.sync.dma_start(out=v2_sb[:], in_=v2)
-        load_seq(0)
-        for k in range(2, X_AHEAD):
+        load_vh(0)
+        w_sb = const.tile([P, 2, C], BF16, name="w_sb")
+        nc.sync.dma_start(out=w_sb[:], in_=W_v.rearrange("(h p) c -> p h c", p=P))
+        load_x(3)
+        load_vf(0)
+        for k in range(4, X_AHEAD):
             load_x(k)
-        load_seq(1)
+        load_vh(1)
+        load_vf(1)
 
         ident_f = const.tile([P, P], F32, name="ident_f")
         make_identity(nc, ident_f[:])
         ident_b = const.tile([P, P], BF16, name="ident_b")
         make_identity(nc, ident_b[:])
-        zeros_f = const.tile([P, P], F32, name="zeros_f")
-        nc.vector.memset(zeros_f[:], 0.0)
 
         xv_ps = psum.tile([P, P], F32, tag="st", bufs=1, name="xv_ps")
         nc.tensor.transpose(xv_ps[:], xv_rows[:], ident_f[:])
@@ -262,12 +270,6 @@ def tile_full_tmix_params_pb_t_kernel(tc, x, x_v, W_v, v_hid, v2, v0, v_first, o
         nc.vector.tensor_scalar(
             out=om[:], in0=m[:], scalar1=-1.0, scalar2=1.0, op0=ALU.mult, op1=ALU.add
         )
-        transpose_wrap(0, 0)
-        transpose_x(0, 0, 0)
-        scale_x(0, 0)
-        transpose_wrap(0, 1)
-        transpose_x(0, 0, 1)
-
         v0_ps = psum.tile([P, P], BF16, tag="st", bufs=1, name="v0_ps")
         nc.tensor.transpose(v0_ps[:], v0_rows[:], ident_b[:])
         v0_col = const.tile([P, 2], F32, name="v0_col")
@@ -275,26 +277,32 @@ def tile_full_tmix_params_pb_t_kernel(tc, x, x_v, W_v, v_hid, v2, v0, v_first, o
         v0_wide = const.tile([P, 2, P], F32, name="v0_wide")
         nc.vector.tensor_copy(out=v0_wide[:], in_=v0_col[:].unsqueeze(2).to_broadcast([P, 2, P]))
 
-        w_words = w_sb[:].bitcast(F32)
-        w_grp = const.tile([P, 2, CO, 4], BF16, name="w_grp", align_bytes=64)
-        w_grp_words = w_grp[:].bitcast(F32)
-        for g in range(2):
-            w_ps = psum.tile([P, 2, 2, P], F32, tag="v", bufs=2, name="w_ps")
-            for u in range(2):
-                for h in range(2):
-                    c0 = (2 * g + u) * P
-                    nc.tensor.transpose(w_ps[:, u, h, :], w_words[:, h, c0 : c0 + P], ident_f[:])
-            nc.vector.tensor_copy(
-                out=w_grp_words[:, g, :, :], in_=w_ps[:].rearrange("p u h r -> p (h r) u")
-            )
+        transpose_x(0, 0, 0)
+        scale_x(0, 0)
+        transpose_wrap(0, 0)
+        transpose_x(0, 0, 1)
+        transpose_wrap(0, 1)
+
         w_codes = const.tile([P, 2 * CO], U32, name="w_codes", align_bytes=64)
         w_scales = const.tile([P, 2 * CO], U8, name="w_scales", align_bytes=64)
-        nc.vector.quantize_mx(
-            out=w_codes[:].bitcast(FP8X4), scales=w_scales[:],
-            in_=w_grp[:].rearrange("p g c t -> p (g c t)"),
-        )
-        transpose_vh(0)
-        copy_vh(0)
+
+        def quantise_w():
+            w_words = w_sb[:].bitcast(F32)
+            w_grp = const.tile([P, 2, CO, 4], BF16, name="w_grp", align_bytes=64)
+            w_grp_words = w_grp[:].bitcast(F32)
+            for g in range(2):
+                w_ps = psum.tile([P, 2, 2, P], F32, tag="v", bufs=2, name="w_ps")
+                for u in range(2):
+                    for h in range(2):
+                        c0 = (2 * g + u) * P
+                        nc.tensor.transpose(w_ps[:, u, h, :], w_words[:, h, c0 : c0 + P], ident_f[:])
+                nc.vector.tensor_copy(
+                    out=w_grp_words[:, g, :, :], in_=w_ps[:].rearrange("p u h r -> p (h r) u")
+                )
+            nc.vector.quantize_mx(
+                out=w_codes[:].bitcast(FP8X4), scales=w_scales[:],
+                in_=w_grp[:].rearrange("p g c t -> p (g c t)"),
+            )
 
         def live(n):
             return 0 <= n < N_STEPS
@@ -311,7 +319,8 @@ def tile_full_tmix_params_pb_t_kernel(tc, x, x_v, W_v, v_hid, v2, v0, v_first, o
             if n + X_AHEAD < N_STEPS:
                 load_x(n + X_AHEAD)
             if n % 4 == 2 and n // 4 + 2 < B:
-                load_seq(n // 4 + 2)
+                load_vh(n // 4 + 2)
+                load_vf(n // 4 + 2)
             if live(n):
                 mix(n, 0)
             if live(n - 1):
@@ -319,11 +328,16 @@ def tile_full_tmix_params_pb_t_kernel(tc, x, x_v, W_v, v_hid, v2, v0, v_first, o
                 sigmoid(n - 1)
             if live(n):
                 refill(n, 0)
+            if n == 0:
+                transpose_vh(0)
+            if live(n):
+                scale_x(n, 1)
+            if n == 0:
+                copy_vh(0)
+            if live(n):
                 gate(n)
             if n % 4 == 1 and n // 4 + 1 < B:
                 transpose_vh(n // 4 + 1)
-            if live(n):
-                scale_x(n, 1)
             if live(n - 3):
                 blend_add(n - 3)
             if live(n - 1):
@@ -342,3 +356,5 @@ def tile_full_tmix_params_pb_t_kernel(tc, x, x_v, W_v, v_hid, v2, v0, v_first, o
                 mix(n, 1)
                 refill(n, 1)
                 regroup_pool(n, 1, 0, NG1)
+            if n == 0:
+                quantise_w()

@@ -16,8 +16,9 @@ B, T, C, CO, DV = 8, 1024, 1024, 256, 128
 FLOPS = 2 * B * T * C * CO + 2 * B * T * DV * CO
 
 N_STEPS = 4 * B
-NG1 = 96
+NG1 = 0
 X_AHEAD = 6
+LOAD_ORDER = (3, 0, 1, 2)
 
 
 def tile_full_tmix_params_pb_t_kernel(tc, x, x_v, W_v, v_hid, v2, v0, v_first, out):
@@ -31,13 +32,10 @@ def tile_full_tmix_params_pb_t_kernel(tc, x, x_v, W_v, v_hid, v2, v0, v_first, o
         psum = ctx.enter_context(tc.psum_pool(name="psum", bufs=1))
         ctx.enter_context(tc.manual_schedule())
 
-        x_loads = [(0, 0), (0, 3), (0, 1), (0, 2)]
-        for b in range(1, B):
-            x_loads.extend([(b, 3), (b, 0), (b, 1), (b, 2)])
         x_tiles = {}
 
         def load_x(k):
-            b, s = x_loads[k]
+            b, s = k // 4, LOAD_ORDER[k % 4]
             if s == 3:
                 x_sb = xin.tile([P, 2, C], BF16, tag="x3", bufs=3, name="x3_sb")
             else:
@@ -48,15 +46,12 @@ def tile_full_tmix_params_pb_t_kernel(tc, x, x_v, W_v, v_hid, v2, v0, v_first, o
 
         seq_tiles = {}
 
-        def load_vh(b):
+        def load_seq(b):
             vh = seqp.tile([P, 8, DV], BF16, name="vh")
             nc.sync.dma_start(out=vh[:], in_=v_hid[b].rearrange("(p j) d -> p j d", j=8))
-            seq_tiles[(b, 0)] = vh
-
-        def load_vf(b):
             vf = seqp.tile([P, 8, CO], BF16, name="vf")
             nc.sync.dma_start(out=vf[:], in_=v_first[b].rearrange("(p j) c -> p j c", j=8))
-            seq_tiles[(b, 1)] = vf
+            seq_tiles[b] = (vh, vf)
 
         banks = {}
         a_tiles = {}
@@ -197,7 +192,7 @@ def tile_full_tmix_params_pb_t_kernel(tc, x, x_v, W_v, v_hid, v2, v0, v_first, o
 
         def blend_sub(n):
             b, s = n // 4, n % 4
-            vf = seq_tiles[(b, 1)][:].rearrange("p (i s) c -> p i s c", s=4)[:, :, s, :]
+            vf = seq_tiles[b][1][:].rearrange("p (i s) c -> p i s c", s=4)[:, :, s, :]
             e_sb = ep.tile([P, 2, CO], F32, name="e_sb")
             nc.vector.tensor_tensor(out=e_sb[:], in0=vf, in1=v_tiles[n][:], op=ALU.subtract)
             e_tiles[n] = e_sb
@@ -221,7 +216,7 @@ def tile_full_tmix_params_pb_t_kernel(tc, x, x_v, W_v, v_hid, v2, v0, v_first, o
         vh_banks = {}
 
         def transpose_vh(b):
-            vh = seq_tiles[(b, 0)]
+            vh = seq_tiles[b][0]
             vh_ps = psum.tile([P, 8, P], BF16, tag="st", bufs=1, name="vh_ps")
             for j in range(8):
                 nc.tensor.transpose(vh_ps[:, j, :], vh[:, j, :], ident_b[:])
@@ -234,33 +229,30 @@ def tile_full_tmix_params_pb_t_kernel(tc, x, x_v, W_v, v_hid, v2, v0, v_first, o
 
         xv_rows = const.tile([P, P], F32, name="xv_rows")
         nc.vector.memset(xv_rows[:], 0.0)
-        v0_rows = const.tile([P, P], BF16, name="v0_rows")
-        nc.vector.memset(v0_rows[:], 0.0)
-        zeros_f = const.tile([P, P], F32, name="zeros_f")
-        nc.vector.memset(zeros_f[:], 0.0)
         nc.sync.dma_start(
             out=xv_rows[:].bitcast(BF16)[0:4, :],
             in_=x_v.rearrange("a b (r c) -> (a b r) c", r=4),
         )
-        nc.sync.dma_start(out=v0_rows[0:2, :], in_=v0.rearrange("a b (h c) -> (a b h) c", h=2))
-        for k in range(3):
-            load_x(k)
-        v2_sb = const.tile([P, CO], BF16, name="v2_sb")
-        nc.sync.dma_start(out=v2_sb[:], in_=v2)
-        load_vh(0)
+        load_x(0)
+        load_x(1)
         w_sb = const.tile([P, 2, C], BF16, name="w_sb")
         nc.sync.dma_start(out=w_sb[:], in_=W_v.rearrange("(h p) c -> p h c", p=P))
-        load_x(3)
-        load_vf(0)
-        for k in range(4, X_AHEAD):
+        v0_rows = const.tile([P, P], BF16, name="v0_rows")
+        nc.vector.memset(v0_rows[:], 0.0)
+        nc.sync.dma_start(out=v0_rows[0:2, :], in_=v0.rearrange("a b (h c) -> (a b h) c", h=2))
+        v2_sb = const.tile([P, CO], BF16, name="v2_sb")
+        nc.sync.dma_start(out=v2_sb[:], in_=v2)
+        load_seq(0)
+        for k in range(2, X_AHEAD):
             load_x(k)
-        load_vh(1)
-        load_vf(1)
+        load_seq(1)
 
         ident_f = const.tile([P, P], F32, name="ident_f")
         make_identity(nc, ident_f[:])
         ident_b = const.tile([P, P], BF16, name="ident_b")
         make_identity(nc, ident_b[:])
+        zeros_f = const.tile([P, P], F32, name="zeros_f")
+        nc.vector.memset(zeros_f[:], 0.0)
 
         xv_ps = psum.tile([P, P], F32, tag="st", bufs=1, name="xv_ps")
         nc.tensor.transpose(xv_ps[:], xv_rows[:], ident_f[:])
@@ -270,6 +262,12 @@ def tile_full_tmix_params_pb_t_kernel(tc, x, x_v, W_v, v_hid, v2, v0, v_first, o
         nc.vector.tensor_scalar(
             out=om[:], in0=m[:], scalar1=-1.0, scalar2=1.0, op0=ALU.mult, op1=ALU.add
         )
+        transpose_wrap(0, 0)
+        transpose_x(0, 0, 0)
+        scale_x(0, 0)
+        transpose_wrap(0, 1)
+        transpose_x(0, 0, 1)
+
         v0_ps = psum.tile([P, P], BF16, tag="st", bufs=1, name="v0_ps")
         nc.tensor.transpose(v0_ps[:], v0_rows[:], ident_b[:])
         v0_col = const.tile([P, 2], F32, name="v0_col")
@@ -277,32 +275,26 @@ def tile_full_tmix_params_pb_t_kernel(tc, x, x_v, W_v, v_hid, v2, v0, v_first, o
         v0_wide = const.tile([P, 2, P], F32, name="v0_wide")
         nc.vector.tensor_copy(out=v0_wide[:], in_=v0_col[:].unsqueeze(2).to_broadcast([P, 2, P]))
 
-        transpose_x(0, 0, 0)
-        scale_x(0, 0)
-        transpose_wrap(0, 0)
-        transpose_x(0, 0, 1)
-        transpose_wrap(0, 1)
-
+        w_words = w_sb[:].bitcast(F32)
+        w_grp = const.tile([P, 2, CO, 4], BF16, name="w_grp", align_bytes=64)
+        w_grp_words = w_grp[:].bitcast(F32)
+        for g in range(2):
+            w_ps = psum.tile([P, 2, 2, P], F32, tag="v", bufs=2, name="w_ps")
+            for u in range(2):
+                for h in range(2):
+                    c0 = (2 * g + u) * P
+                    nc.tensor.transpose(w_ps[:, u, h, :], w_words[:, h, c0 : c0 + P], ident_f[:])
+            nc.vector.tensor_copy(
+                out=w_grp_words[:, g, :, :], in_=w_ps[:].rearrange("p u h r -> p (h r) u")
+            )
         w_codes = const.tile([P, 2 * CO], U32, name="w_codes", align_bytes=64)
         w_scales = const.tile([P, 2 * CO], U8, name="w_scales", align_bytes=64)
-
-        def quantise_w():
-            w_words = w_sb[:].bitcast(F32)
-            w_grp = const.tile([P, 2, CO, 4], BF16, name="w_grp", align_bytes=64)
-            w_grp_words = w_grp[:].bitcast(F32)
-            for g in range(2):
-                w_ps = psum.tile([P, 2, 2, P], F32, tag="v", bufs=2, name="w_ps")
-                for u in range(2):
-                    for h in range(2):
-                        c0 = (2 * g + u) * P
-                        nc.tensor.transpose(w_ps[:, u, h, :], w_words[:, h, c0 : c0 + P], ident_f[:])
-                nc.vector.tensor_copy(
-                    out=w_grp_words[:, g, :, :], in_=w_ps[:].rearrange("p u h r -> p (h r) u")
-                )
-            nc.vector.quantize_mx(
-                out=w_codes[:].bitcast(FP8X4), scales=w_scales[:],
-                in_=w_grp[:].rearrange("p g c t -> p (g c t)"),
-            )
+        nc.vector.quantize_mx(
+            out=w_codes[:].bitcast(FP8X4), scales=w_scales[:],
+            in_=w_grp[:].rearrange("p g c t -> p (g c t)"),
+        )
+        transpose_vh(0)
+        copy_vh(0)
 
         def live(n):
             return 0 <= n < N_STEPS
@@ -319,8 +311,7 @@ def tile_full_tmix_params_pb_t_kernel(tc, x, x_v, W_v, v_hid, v2, v0, v_first, o
             if n + X_AHEAD < N_STEPS:
                 load_x(n + X_AHEAD)
             if n % 4 == 2 and n // 4 + 2 < B:
-                load_vh(n // 4 + 2)
-                load_vf(n // 4 + 2)
+                load_seq(n // 4 + 2)
             if live(n):
                 mix(n, 0)
             if live(n - 1):
@@ -328,16 +319,11 @@ def tile_full_tmix_params_pb_t_kernel(tc, x, x_v, W_v, v_hid, v2, v0, v_first, o
                 sigmoid(n - 1)
             if live(n):
                 refill(n, 0)
-            if n == 0:
-                transpose_vh(0)
-            if live(n):
-                scale_x(n, 1)
-            if n == 0:
-                copy_vh(0)
-            if live(n):
                 gate(n)
             if n % 4 == 1 and n // 4 + 1 < B:
                 transpose_vh(n // 4 + 1)
+            if live(n):
+                scale_x(n, 1)
             if live(n - 3):
                 blend_add(n - 3)
             if live(n - 1):
@@ -355,6 +341,5 @@ def tile_full_tmix_params_pb_t_kernel(tc, x, x_v, W_v, v_hid, v2, v0, v_first, o
             if live(n):
                 mix(n, 1)
                 refill(n, 1)
-                regroup_pool(n, 1, 0, NG1)
-            if n == 0:
-                quantise_w()
+                if NG1 > 0:
+                    regroup_pool(n, 1, 0, NG1)

@@ -16,7 +16,8 @@ B, T, C, CO, DV = 8, 1024, 1024, 256, 128
 FLOPS = 2 * B * T * C * CO + 2 * B * T * DV * CO
 
 N_STEPS = 4 * B
-NG1 = 0
+NG1 = 32
+NV1 = 32
 X_AHEAD = 6
 LOAD_ORDER = (3, 0, 1, 2)
 
@@ -129,6 +130,13 @@ def tile_full_tmix_params_pb_t_kernel(tc, x, x_v, W_v, v_hid, v2, v0, v_first, o
         def regroup_act(n, g, lo, hi):
             src = xvp_tiles[n][:].rearrange("p (g t) i r -> p g t (i r)", g=2)
             nc.scalar.copy(
+                out=grp_tiles[n][:, g, lo:hi, :].rearrange("p (c i) t -> p c t i", i=4),
+                in_=src[:, g, :, lo:hi].rearrange("p t (c i) -> p c t i", i=4),
+            )
+
+        def regroup_vec(n, g, lo, hi):
+            src = xvp_tiles[n][:].rearrange("p (g t) i r -> p g t (i r)", g=2)
+            nc.vector.tensor_copy(
                 out=grp_tiles[n][:, g, lo:hi, :].rearrange("p (c i) t -> p c t i", i=4),
                 in_=src[:, g, :, lo:hi].rearrange("p t (c i) -> p c t i", i=4),
             )
@@ -315,7 +323,7 @@ def tile_full_tmix_params_pb_t_kernel(tc, x, x_v, W_v, v_hid, v2, v0, v_first, o
             if live(n):
                 mix(n, 0)
             if live(n - 1):
-                regroup_act(n - 1, 1, NG1, 2 * P)
+                regroup_act(n - 1, 1, NG1 + NV1, 2 * P)
                 sigmoid(n - 1)
             if live(n):
                 refill(n, 0)
@@ -327,6 +335,7 @@ def tile_full_tmix_params_pb_t_kernel(tc, x, x_v, W_v, v_hid, v2, v0, v_first, o
             if live(n - 3):
                 blend_add(n - 3)
             if live(n - 1):
+                regroup_vec(n - 1, 1, NG1, NG1 + NV1)
                 quantise(n - 1)
                 project(n - 1)
             if live(n):
@@ -341,5 +350,4 @@ def tile_full_tmix_params_pb_t_kernel(tc, x, x_v, W_v, v_hid, v2, v0, v_first, o
             if live(n):
                 mix(n, 1)
                 refill(n, 1)
-                if NG1 > 0:
-                    regroup_pool(n, 1, 0, NG1)
+                regroup_pool(n, 1, 0, NG1)

from contextlib import ExitStack

import concourse.mybir as mybir
from concourse.masks import make_identity

FP8X4 = mybir.dt.float8_e4m3fn_x4
BF16 = mybir.dt.bfloat16
F32 = mybir.dt.float32
U32 = mybir.dt.uint32
U8 = mybir.dt.uint8
ALU = mybir.AluOpType
ACT = mybir.ActivationFunctionType

P = 128
B, T, C, CO, DV = 8, 1024, 1024, 256, 128
FLOPS = 2 * B * T * C * CO + 2 * B * T * DV * CO

N_STEPS = 4 * B
NG1 = 32
NV1 = 32
X_AHEAD = 6
LOAD_ORDER = (3, 0, 1, 2)


def tile_full_tmix_params_pb_t_kernel(tc, x, x_v, W_v, v_hid, v2, v0, v_first, out):
    nc = tc.nc
    with ExitStack() as ctx:
        const = ctx.enter_context(tc.tile_pool(name="const", bufs=1))
        xin = ctx.enter_context(tc.tile_pool(name="xin", bufs=1))
        seqp = ctx.enter_context(tc.tile_pool(name="seqp", bufs=3))
        work = ctx.enter_context(tc.tile_pool(name="work", bufs=3))
        ep = ctx.enter_context(tc.tile_pool(name="ep", bufs=3))
        psum = ctx.enter_context(tc.psum_pool(name="psum", bufs=1))
        ctx.enter_context(tc.manual_schedule())

        x_tiles = {}

        def load_x(k):
            b, s = k // 4, LOAD_ORDER[k % 4]
            if s == 3:
                x_sb = xin.tile([P, 2, C], BF16, tag="x3", bufs=3, name="x3_sb")
            else:
                x_sb = xin.tile([P, 2, C], BF16, tag="x", bufs=6, name="x_sb")
            src = x[b].rearrange("(p i s) c -> p i s c", i=2, s=4)
            nc.sync.dma_start(out=x_sb[:], in_=src[:, :, s, :])
            x_tiles[(b, s)] = x_sb

        seq_tiles = {}

        def load_seq(b):
            vh = seqp.tile([P, 8, DV], BF16, name="vh")
            nc.sync.dma_start(out=vh[:], in_=v_hid[b].rearrange("(p j) d -> p j d", j=8))
            vf = seqp.tile([P, 8, CO], BF16, name="vf")
            nc.sync.dma_start(out=vf[:], in_=v_first[b].rearrange("(p j) c -> p j c", j=8))
            seq_tiles[b] = (vh, vf)

        banks = {}
        a_tiles = {}

        def bank_tile(g):
            if g == 0:
                return psum.tile([P, 2, 2, P], F32, tag="xt0", bufs=2, name="xt0_ps")
            return psum.tile([P, 2, 2, P], F32, tag="xt1", bufs=2, name="xt1_ps")

        def as_planes(bk):
            return bk[:].bitcast(BF16).rearrange("p u i (r e) -> p u i r e", e=2)

        def transpose_x(b, s, g):
            xw = x_tiles[(b, s)][:].bitcast(F32)
            bk = bank_tile(g)
            for u in range(2):
                for i in range(2):
                    c0 = (2 * g + u) * P
                    nc.tensor.transpose(bk[:, u, i, :], xw[:, i, c0 : c0 + P], ident_f[:])
            banks[(b, s, g)] = as_planes(bk)

        def transpose_wrap(b, g):
            xw = x_tiles[(b, 3)][:].bitcast(F32)
            bk = bank_tile(g)
            for u in range(2):
                c0 = (2 * g + u) * P
                row = bk[:, u, :, :].rearrange("p i r -> p (i r)")
                nc.tensor.transpose(row[:, 0:P], zeros_f[:], ident_f[:])
                nc.tensor.transpose(row[:, 1 : P + 1], xw[:, 1, c0 : c0 + P], ident_f[:])
                nc.tensor.transpose(row[:, P : 2 * P], xw[:, 0, c0 : c0 + P], ident_f[:])
            banks[(b, -1, g)] = as_planes(bk)

        def scale_x(n, g):
            key = (n // 4, n % 4)
            if g == 0:
                a_tiles[key] = work.tile([P, 8, 2, P], F32, name="a")
            a = a_tiles[key]
            bv = banks[(key[0], key[1], g)]
            for u in range(2):
                for e in range(2):
                    pl = 4 * g + 2 * u + e
                    nc.scalar.activation(
                        out=a[:, pl, :, :], in_=bv[:, u, :, :, e], func=ACT.Copy,
                        scale=om[:, pl : pl + 1],
                    )

        xvp_tiles = {}

        def mix(n, g):
            b, s = n // 4, n % 4
            prev = banks[(b, s - 1, g)]
            a = a_tiles[(b, s)]
            if g == 0:
                xvp_tiles[n] = work.tile([P, 8, 2, P], BF16, name="xvp")
            xvp = xvp_tiles[n]
            for u in range(2):
                for e in range(2):
                    pl = 4 * g + 2 * u + e
                    nc.vector.scalar_tensor_tensor(
                        out=xvp[:, pl, :, :], in0=prev[:, u, :, :, e], scalar=m[:, pl : pl + 1],
                        in1=a[:, pl, :, :], op0=ALU.mult, op1=ALU.add,
                    )

        grp_tiles = {}

        def regroup_pool(n, g, lo, hi):
            if g == 0:
                grp_tiles[n] = work.tile([P, 2, 2 * P, 4], BF16, tag="grp", bufs=1, name="grp", align_bytes=64)
            src = xvp_tiles[n][:].rearrange("p (g t) i r -> p g (i r) t", g=2)
            nc.gpsimd.tensor_scalar(
                out=grp_tiles[n][:, g, lo:hi, :], in0=src[:, g, lo:hi, :], scalar1=1.0, scalar2=0.0,
                op0=ALU.mult, op1=ALU.add,
            )

        def regroup_act(n, g, lo, hi):
            src = xvp_tiles[n][:].rearrange("p (g t) i r -> p g t (i r)", g=2)
            nc.scalar.copy(
                out=grp_tiles[n][:, g, lo:hi, :].rearrange("p (c i) t -> p c t i", i=4),
                in_=src[:, g, :, lo:hi].rearrange("p t (c i) -> p c t i", i=4),
            )

        def regroup_vec(n, g, lo, hi):
            src = xvp_tiles[n][:].rearrange("p (g t) i r -> p g t (i r)", g=2)
            nc.vector.tensor_copy(
                out=grp_tiles[n][:, g, lo:hi, :].rearrange("p (c i) t -> p c t i", i=4),
                in_=src[:, g, :, lo:hi].rearrange("p t (c i) -> p c t i", i=4),
            )

        g_tiles = {}

        def gate(n):
            b, s = n // 4, n % 4
            vht = vht_tiles[b]
            g_ps = psum.tile([P, 2, CO], F32, tag="g", bufs=1, name="g_ps")
            for i in range(2):
                for h in range(2):
                    nc.tensor.matmul(
                        out=g_ps[:, i, h * P : (h + 1) * P], lhsT=v0_wide[:, h, :], rhs=ident_f[:],
                        is_transpose=True, start=(h == 0), stop=False,
                    )
                nc.tensor.matmul(
                    out=g_ps[:, i, :], lhsT=vht[:, 4 * i + s, :], rhs=v2_sb[:], start=False, stop=True
                )
            g_tiles[n] = g_ps

        mix_tiles = {}

        def sigmoid(n):
            mx_t = ep.tile([P, 2, CO], F32, name="mix_sb")
            nc.scalar.activation(out=mx_t[:], in_=g_tiles[n][:], func=ACT.Sigmoid)
            mix_tiles[n] = mx_t

        q_tiles = {}

        def quantise(n):
            xc = work.tile([P, 4 * P], U32, name="xc", align_bytes=64)
            xs = work.tile([P, 4 * P], U8, name="xs", align_bytes=64)
            nc.vector.quantize_mx(
                out=xc[:].bitcast(FP8X4), scales=xs[:],
                in_=grp_tiles[n][:].rearrange("p g n t -> p (g n t)"),
            )
            q_tiles[n] = (xc, xs)

        v_tiles = {}

        def project(n):
            xc, xs = q_tiles[n]
            v_ps = psum.tile([P, 2, CO], F32, tag="v", bufs=2, name="v_ps")
            for i in range(2):
                for g in range(2):
                    c0 = g * 2 * P + i * P
                    nc.tensor.matmul_mx(
                        out=v_ps[:, i, :],
                        lhsT=xc[:, c0 : c0 + P].bitcast(FP8X4),
                        lhsT_scale=xs[:, c0 : c0 + P],
                        rhs=w_codes[:, g * CO : (g + 1) * CO].bitcast(FP8X4),
                        rhs_scale=w_scales[:, g * CO : (g + 1) * CO],
                        start=(g == 0),
                        stop=(g == 1),
                    )
            v_tiles[n] = v_ps

        e_tiles = {}
        f_tiles = {}

        def blend_sub(n):
            b, s = n // 4, n % 4
            vf = seq_tiles[b][1][:].rearrange("p (i s) c -> p i s c", s=4)[:, :, s, :]
            e_sb = ep.tile([P, 2, CO], F32, name="e_sb")
            nc.vector.tensor_tensor(out=e_sb[:], in0=vf, in1=v_tiles[n][:], op=ALU.subtract)
            e_tiles[n] = e_sb

        def blend_mul(n):
            f_sb = ep.tile([P, 2, CO], F32, name="f_sb")
            if n < N_STEPS - 2:
                nc.gpsimd.tensor_tensor(out=f_sb[:], in0=e_tiles[n][:], in1=mix_tiles[n][:], op=ALU.mult)
            else:
                nc.vector.tensor_tensor(out=f_sb[:], in0=e_tiles[n][:], in1=mix_tiles[n][:], op=ALU.mult)
            f_tiles[n] = f_sb

        def blend_add(n):
            b, s = n // 4, n % 4
            o_sb = ep.tile([P, 2, CO], F32, name="o_sb")
            nc.vector.tensor_tensor(out=o_sb[:], in0=f_tiles[n][:], in1=v_tiles[n][:], op=ALU.add)
            dst = out[b].rearrange("(p i s) c -> p i s c", i=2, s=4)
            nc.sync.dma_start(out=dst[:, :, s, :], in_=o_sb[:])

        vht_tiles = {}
        vh_banks = {}

        def transpose_vh(b):
            vh = seq_tiles[b][0]
            vh_ps = psum.tile([P, 8, P], BF16, tag="st", bufs=1, name="vh_ps")
            for j in range(8):
                nc.tensor.transpose(vh_ps[:, j, :], vh[:, j, :], ident_b[:])
            vh_banks[b] = vh_ps

        def copy_vh(b):
            vht = seqp.tile([P, 8, P], BF16, name="vht")
            nc.scalar.copy(out=vht[:], in_=vh_banks[b][:])
            vht_tiles[b] = vht

        xv_rows = const.tile([P, P], F32, name="xv_rows")
        nc.vector.memset(xv_rows[:], 0.0)
        nc.sync.dma_start(
            out=xv_rows[:].bitcast(BF16)[0:4, :],
            in_=x_v.rearrange("a b (r c) -> (a b r) c", r=4),
        )
        load_x(0)
        load_x(1)
        w_sb = const.tile([P, 2, C], BF16, name="w_sb")
        nc.sync.dma_start(out=w_sb[:], in_=W_v.rearrange("(h p) c -> p h c", p=P))
        v0_rows = const.tile([P, P], BF16, name="v0_rows")
        nc.vector.memset(v0_rows[:], 0.0)
        nc.sync.dma_start(out=v0_rows[0:2, :], in_=v0.rearrange("a b (h c) -> (a b h) c", h=2))
        v2_sb = const.tile([P, CO], BF16, name="v2_sb")
        nc.sync.dma_start(out=v2_sb[:], in_=v2)
        load_seq(0)
        for k in range(2, X_AHEAD):
            load_x(k)
        load_seq(1)

        ident_f = const.tile([P, P], F32, name="ident_f")
        make_identity(nc, ident_f[:])
        ident_b = const.tile([P, P], BF16, name="ident_b")
        make_identity(nc, ident_b[:])
        zeros_f = const.tile([P, P], F32, name="zeros_f")
        nc.vector.memset(zeros_f[:], 0.0)

        xv_ps = psum.tile([P, P], F32, tag="st", bufs=1, name="xv_ps")
        nc.tensor.transpose(xv_ps[:], xv_rows[:], ident_f[:])
        m = const.tile([P, 8], F32, name="m")
        nc.vector.tensor_copy(out=m[:], in_=xv_ps[:, 0:4].bitcast(BF16))
        om = const.tile([P, 8], F32, name="om")
        nc.vector.tensor_scalar(
            out=om[:], in0=m[:], scalar1=-1.0, scalar2=1.0, op0=ALU.mult, op1=ALU.add
        )
        transpose_wrap(0, 0)
        transpose_x(0, 0, 0)
        scale_x(0, 0)
        transpose_wrap(0, 1)
        transpose_x(0, 0, 1)

        v0_ps = psum.tile([P, P], BF16, tag="st", bufs=1, name="v0_ps")
        nc.tensor.transpose(v0_ps[:], v0_rows[:], ident_b[:])
        v0_col = const.tile([P, 2], F32, name="v0_col")
        nc.vector.tensor_copy(out=v0_col[:], in_=v0_ps[:, 0:2])
        v0_wide = const.tile([P, 2, P], F32, name="v0_wide")
        nc.vector.tensor_copy(out=v0_wide[:], in_=v0_col[:].unsqueeze(2).to_broadcast([P, 2, P]))

        w_words = w_sb[:].bitcast(F32)
        w_grp = const.tile([P, 2, CO, 4], BF16, name="w_grp", align_bytes=64)
        w_grp_words = w_grp[:].bitcast(F32)
        for g in range(2):
            w_ps = psum.tile([P, 2, 2, P], F32, tag="v", bufs=2, name="w_ps")
            for u in range(2):
                for h in range(2):
                    c0 = (2 * g + u) * P
                    nc.tensor.transpose(w_ps[:, u, h, :], w_words[:, h, c0 : c0 + P], ident_f[:])
            nc.vector.tensor_copy(
                out=w_grp_words[:, g, :, :], in_=w_ps[:].rearrange("p u h r -> p (h r) u")
            )
        w_codes = const.tile([P, 2 * CO], U32, name="w_codes", align_bytes=64)
        w_scales = const.tile([P, 2 * CO], U8, name="w_scales", align_bytes=64)
        nc.vector.quantize_mx(
            out=w_codes[:].bitcast(FP8X4), scales=w_scales[:],
            in_=w_grp[:].rearrange("p g c t -> p (g c t)"),
        )
        transpose_vh(0)
        copy_vh(0)

        def live(n):
            return 0 <= n < N_STEPS

        def refill(n, g):
            b, s = n // 4, n % 4
            if s < 3:
                transpose_x(b, s + 1, g)
            elif b + 1 < B:
                transpose_x(b + 1, 0, g)
                transpose_wrap(b + 1, g)

        for n in range(N_STEPS + 3):
            if n + X_AHEAD < N_STEPS:
                load_x(n + X_AHEAD)
            if n % 4 == 2 and n // 4 + 2 < B:
                load_seq(n // 4 + 2)
            if live(n):
                mix(n, 0)
            if live(n - 1):
                regroup_act(n - 1, 1, NG1 + NV1, 2 * P)
                sigmoid(n - 1)
            if live(n):
                refill(n, 0)
                gate(n)
            if n % 4 == 1 and n // 4 + 1 < B:
                transpose_vh(n // 4 + 1)
            if live(n):
                scale_x(n, 1)
            if live(n - 3):
                blend_add(n - 3)
            if live(n - 1):
                regroup_vec(n - 1, 1, NG1, NG1 + NV1)
                quantise(n - 1)
                project(n - 1)
            if live(n):
                regroup_pool(n, 0, 0, 2 * P)
            if live(n - 2):
                blend_sub(n - 2)
                blend_mul(n - 2)
            if live(n + 1):
                scale_x(n + 1, 0)
            if n % 4 == 1 and n // 4 + 1 < B:
                copy_vh(n // 4 + 1)
            if live(n):
                mix(n, 1)
                refill(n, 1)
                regroup_pool(n, 1, 0, NG1)
